import numpy as np
import ml_dtypes


def mxq(x, axis, fmt="e4m3"):
    dtype, down = {"e4m3": (ml_dtypes.float8_e4m3fn, 7), "e5m2": (ml_dtypes.float8_e5m2, 14)}[fmt]
    v = np.moveaxis(np.asarray(x, np.float32).astype(ml_dtypes.bfloat16).astype(np.float64), axis, -1)
    blocks = v.reshape(v.shape[:-1] + (-1, 32))
    amax = np.abs(blocks).max(-1, keepdims=True)
    byte = np.maximum(np.where(amax > 0, np.frexp(amax)[1] - 1 + 127, 0) - down, 1)
    scale = np.exp2(byte - 127.0)
    codes = (blocks / scale).astype(np.float32).astype(dtype).astype(np.float64)
    return np.moveaxis((codes * scale).reshape(v.shape), -1, axis)


WIDE = False


def mx_kscale(k):
    if not WIDE:
        return np.ones(k)
    levels = np.array([10, -10, 5, -5, 0])
    if k % 512:
        return np.exp2(np.random.permutation(np.resize(levels, k // 32))).repeat(32)
    a = np.empty((k // 512, 16))
    for p in range(k // 512):
        a[p, :8] = np.random.permutation(np.resize(levels, 8))
        for g in range(8):
            far = levels[np.abs(levels - a[p, g]) >= 10]
            a[p, g + 8] = far[np.random.randint(len(far))]
    return np.exp2(a.ravel()).repeat(32)


BF16 = ml_dtypes.bfloat16


def bf(x):
    return np.asarray(x, np.float32).astype(BF16)


def f64(x):
    return np.asarray(x).astype(np.float64)


B, T, H, W, C, NH, RD = 2, 4, 8, 16, 1024, 16, 16
N = T * H * W
HD = C // NH
ROT = 3 * RD
MAX_FREQ = 256.0


def axis_freqs(n):
    base = np.linspace(1.0, MAX_FREQ / 2.0, RD // 2) * np.pi
    pos = np.linspace(-1.0, 1.0, n)
    return np.repeat(pos[:, None] * base[None, :], 2, axis=-1)


def axial_freqs():
    ft = np.broadcast_to(axis_freqs(T)[:, None, None, :], (T, H, W, RD))
    fh = np.broadcast_to(axis_freqs(H)[None, :, None, :], (T, H, W, RD))
    fw = np.broadcast_to(axis_freqs(W)[None, None, :, :], (T, H, W, RD))
    return np.concatenate([ft, fh, fw], axis=-1)


def rotate_half(v):
    p = v.reshape(*v.shape[:-1], -1, 2)
    return np.stack([-p[..., 1], p[..., 0]], axis=-1).reshape(v.shape)


def apply_rope(freqs, t):
    tm, tr = t[..., :ROT], t[..., ROT:]
    tm = tm * np.cos(freqs) + rotate_half(tm) * np.sin(freqs)
    return np.concatenate([tm, tr], axis=-1)


def draw0():
    s = mx_kscale(C)
    return {'x': bf(np.random.standard_normal((B, N, C)) * s),
            'Wqkv': bf(np.random.standard_normal((C, 3 * C)) * 0.6 / np.sqrt(C) / s[:, None])}


def core(x, Wqkv):
    qkv = mxq(f64(x), 2, 'e4m3') @ mxq(f64(Wqkv), 0, 'e4m3')
    qkv = qkv.reshape(B, N, 3, NH, HD).transpose(2, 0, 3, 1, 4)
    q, k, v = qkv[0], qkv[1], qkv[2]
    freqs = axial_freqs()
    q_rot = apply_rope(freqs, q.reshape(B, NH, T, H, W, HD)).reshape(B, NH, N, HD)
    k_rot = apply_rope(freqs, k.reshape(B, NH, T, H, W, HD)).reshape(B, NH, N, HD)
    return q_rot, k_rot, v


def e4m3fn_bytes(y):
    return np.clip(np.asarray(y, np.float64), -448.0, 448.0).astype(np.float32).astype(ml_dtypes.float8_e4m3fn).view(np.uint8)


def e4m3fn_values(b):
    return np.asarray(b, np.uint8).view(ml_dtypes.float8_e4m3fn).astype(np.float64)


def setup_inputs():
    d = draw0()
    x0 = np.asarray(d['Wqkv']).astype(np.float64)
    s = (np.max(np.abs(x0), axis=(1,), keepdims=True) / 448.0).astype(np.float32)
    out = {}
    for k, v in d.items():
        if k == 'Wqkv':
            out['Wqkv_bytes'] = e4m3fn_bytes(x0 / s.astype(np.float64))
            out['Wqkv_scale'] = s
        else:
            out[k] = v
    return out


def reference(x, Wqkv_bytes, Wqkv_scale):
    return core(x, e4m3fn_values(Wqkv_bytes) * Wqkv_scale.astype(np.float64))

@@ -1,0 +1,328 @@
+from contextlib import ExitStack
+import math
+
+import concourse.mybir as mybir
+from concourse.masks import make_identity
+
+FLOPS = 2 * 1024 * 1024 * 3072
+
+F32 = mybir.dt.float32
+BF16 = mybir.dt.bfloat16
+U32 = mybir.dt.uint32
+U8 = mybir.dt.uint8
+I32 = mybir.dt.int32
+FP8 = mybir.dt.float8_e4m3fn
+FP8X4 = mybir.dt.float8_e4m3fn_x4
+ALU = mybir.AluOpType
+ACT = mybir.ActivationFunctionType
+
+P = 128
+NCH = 6
+CW = 512
+LOOKAHEAD = 2
+WIDEN_ON_V = ((0, 1),)
+V_AFTER = (12, 13, 14, 15, 16, 17, 18, 19, 20, 21, 22, 23, 24, 25, 26, 27)
+PASS_ON_V = True
+XCOPY_ON_V = (5,)
+TB_BUFS = 4
+OT_BUFS = 5
+S_PACE = 1
+V_PACE = 2
+SPLIT_UNITS = ((3, 1),)
+
+
+def make_jobs():
+    v_jobs = []
+    for c in (4, 5):
+        for b in range(2):
+            for i in range(4):
+                v_jobs.append((c, b, i))
+    jobs = []
+    n = 0
+    nv = 0
+    for c in range(4):
+        for b in range(2):
+            for i in range(4):
+                jobs.append((c, b, i))
+                if n in V_AFTER:
+                    jobs.append(v_jobs[nv])
+                    nv += 1
+                n += 1
+    assert nv == 16
+    return jobs
+
+S_IL = ((2, 0), (5, 0), (3, 0))
+V_ADDS = ((3, 1, 2), (3, 1, 3))
+
+
+def tile_attention_pa_kernel(tc, x, Wqkv_bytes, Wqkv_scale, out_0, out_1, out_2):
+    nc = tc.nc
+    outs = (out_0, out_1, out_2)
+    jobs = make_jobs()
+    first_use = {}
+    for k in range(len(jobs)):
+        first_use.setdefault(jobs[k][0], k)
+    PREP_ORDER = tuple(sorted(range(NCH), key=lambda c: first_use[c]))
+
+    with ExitStack() as ctx:
+        const = ctx.enter_context(tc.tile_pool(name="const", bufs=1))
+        xgp = ctx.enter_context(tc.tile_pool(name="xgp", bufs=3))
+        wplp = ctx.enter_context(tc.tile_pool(name="wplp", bufs=3))
+        wgp = ctx.enter_context(tc.tile_pool(name="wgp", bufs=2))
+        otp = ctx.enter_context(tc.tile_pool(name="otp", bufs=OT_BUFS))
+        tbp = ctx.enter_context(tc.tile_pool(name="tbp", bufs=TB_BUFS))
+        psx = ctx.enter_context(tc.psum_pool(name="psx", bufs=2))
+        psa = ctx.enter_context(tc.psum_pool(name="psa", bufs=6))
+
+        ws = const.tile([P, 2, 4], F32, name="ws")
+        nc.sync.dma_start(out=ws[:], in_=Wqkv_scale.rearrange("(g p t) o -> p g (t o)", p=P, t=4))
+        wview = Wqkv_bytes.rearrange("(g p t) n -> g p t n", p=P, t=4)
+        wb = []
+        for c in range(NCH):
+            wb.append(const.tile([P, 2, 4, CW], U8, name="wb%d" % c))
+        xsb = []
+        for b in range(2):
+            xsb.append(const.tile([P, 4, 1024], BF16, name="xsb%d" % b))
+
+        def load_w(c):
+            for g in range(2):
+                nc.sync.dma_start(out=wb[c][:, g], in_=wview[g][:, :, c * CW:(c + 1) * CW])
+
+        def load_x(b):
+            xv = x[b].rearrange("(p i) k -> p i k", i=4)
+            for h in range(2):
+                nc.sync.dma_start(out=xsb[b][:, 2 * h:2 * h + 2, :], in_=xv[:, 2 * h:2 * h + 2, :])
+
+        load_w(PREP_ORDER[0])
+        load_x(0)
+        load_w(PREP_ORDER[1])
+        load_x(1)
+        for c in PREP_ORDER[2:]:
+            load_w(c)
+
+        zero = const.tile([P, 8], F32, name="zero")
+        nc.vector.memset(zero[:], 0.0)
+        warm = const.tile([P, 8], F32, name="warm")
+        nc.scalar.activation(out=warm[:], in_=zero[:], func=ACT.Sin)
+
+        ident = const.tile([P, P], F32, name="ident")
+        make_identity(nc, ident[:])
+
+        pi = const.tile([P, 1], I32, name="pi")
+        nc.gpsimd.iota(pi[:], pattern=[[0, 1]], base=0, channel_multiplier=1)
+        fq = const.tile([P, 2, 16], F32, name="fq")
+        nc.gpsimd.iota(fq[:, 0, :], pattern=[[127, 8], [0, 2]], base=7, channel_multiplier=0,
+                       allow_small_or_imprecise_dtypes=True)
+        sg = const.tile([P, 16], F32, name="sg")
+        nc.gpsimd.iota(sg[:], pattern=[[0, 8], [2, 2]], base=-1, channel_multiplier=0,
+                       allow_small_or_imprecise_dtypes=True)
+        i28 = const.tile([P, 4], F32, name="i28")
+        nc.gpsimd.iota(i28[:], pattern=[[28, 4]], base=-210, channel_multiplier=0,
+                       allow_small_or_imprecise_dtypes=True)
+        nc.vector.tensor_tensor(out=fq[:, 1, :], in0=fq[:, 0, :], in1=sg[:], op=ALU.mult)
+        idx = const.tile([P, 3], I32, name="idx")
+        nc.vector.tensor_scalar(out=idx[:, 0:1], in0=pi[:], scalar1=5, scalar2=None,
+                                op0=ALU.logical_shift_right)
+        nc.vector.tensor_scalar(out=idx[:, 1:2], in0=pi[:], scalar1=2, scalar2=7,
+                                op0=ALU.logical_shift_right, op1=ALU.bitwise_and)
+        nc.vector.tensor_scalar(out=idx[:, 2:3], in0=pi[:], scalar1=3, scalar2=None,
+                                op0=ALU.bitwise_and)
+        idf = const.tile([P, 3], F32, name="idf")
+        nc.vector.tensor_copy(out=idf[:], in_=idx[:])
+        mm = const.tile([P, 6], F32, name="mm")
+        nc.vector.tensor_scalar(out=mm[:, 0:1], in0=idf[:, 0:1], scalar1=140.0, scalar2=-210.0,
+                                op0=ALU.mult, op1=ALU.add)
+        nc.vector.tensor_scalar(out=mm[:, 1:2], in0=idf[:, 1:2], scalar1=60.0, scalar2=-210.0,
+                                op0=ALU.mult, op1=ALU.add)
+        nc.vector.scalar_tensor_tensor(out=mm[:, 2:6], in0=idf[:, 2:3].to_broadcast([P, 4]),
+                                       scalar=112.0, in1=i28[:], op0=ALU.mult, op1=ALU.add)
+        nn = const.tile([P, 2, 6, 16], F32, name="nn")
+        nc.vector.tensor_tensor(out=nn[:],
+                                in0=mm[:].unsqueeze(1).unsqueeze(3).to_broadcast([P, 2, 6, 16]),
+                                in1=fq[:].unsqueeze(2).to_broadcast([P, 2, 6, 16]), op=ALU.mult)
+        nc.vector.tensor_scalar(out=nn[:, 0], in0=nn[:, 0], scalar1=191835.0, scalar2=None, op0=ALU.add)
+        nc.vector.tensor_scalar(out=nn[:, 1], in0=nn[:, 1], scalar1=191100.0, scalar2=None, op0=ALU.add)
+        nflat = nn[:].rearrange("p a s d -> p (a s d)")
+        qi = const.tile([P, 192], I32, name="qi")
+        nc.vector.tensor_scalar(out=qi[:], in0=nflat, scalar1=1.0 / 2940.0, scalar2=None, op0=ALU.mult)
+        rr = const.tile([P, 192], F32, name="rr")
+        nc.vector.scalar_tensor_tensor(out=rr[:], in0=qi[:], scalar=-2940.0, in1=nflat,
+                                       op0=ALU.mult, op1=ALU.add)
+        t1 = const.tile([P, 192], F32, name="t1")
+        nc.vector.tensor_scalar(out=t1[:], in0=rr[:], scalar1=-1.0, scalar2=1470.0,
+                                op0=ALU.mult, op1=ALU.add)
+        t2 = const.tile([P, 192], F32, name="t2")
+        nc.vector.tensor_tensor(out=t2[:], in0=rr[:], in1=t1[:], op=ALU.min)
+        t3 = const.tile([P, 192], F32, name="t3")
+        nc.vector.scalar_tensor_tensor(out=t3[:], in0=t1[:], scalar=-2940.0, in1=t2[:],
+                                       op0=ALU.add, op1=ALU.max)
+        t4 = const.tile([P, 2, 6, 16], F32, name="t4")
+        nc.vector.scalar_tensor_tensor(out=t4[:].rearrange("p a s d -> p (a s d)"), in0=rr[:],
+                                       scalar=-2940.0, in1=t3[:], op0=ALU.add, op1=ALU.max)
+        tabs = []
+        for a in range(2):
+            tab = const.tile([P, 4, 64], F32, name="tab%d" % a)
+            nc.vector.memset(tab[:, :, 48:64], 1.0)
+            nc.scalar.activation(out=tab[:, :, 0:32],
+                                 in_=t4[:, a, 0:2, :].rearrange("p s d -> p (s d)").unsqueeze(1)
+                                 .to_broadcast([P, 4, 32]),
+                                 func=ACT.Sin, scale=math.pi / 1470.0)
+            nc.scalar.activation(out=tab[:, :, 32:48], in_=t4[:, a, 2:6, :],
+                                 func=ACT.Sin, scale=math.pi / 1470.0)
+            tabs.append(tab)
+        ctab, stab = tabs
+
+        xc = const.tile([P, 8, 256], U32, name="xc", align_bytes=64)
+        xs = const.tile([P, 8, 256], U8, name="xs", align_bytes=64)
+
+        def prep_x(b, i):
+            m = 4 * b + i
+            words = xsb[b][:, i, :].bitcast(F32)
+            xt = psx.tile([P, 4, P], F32, name="xt")
+            for g in range(2):
+                for u in range(2):
+                    nc.tensor.transpose(xt[:, 2 * g + u, :],
+                                        words[:, 256 * g + u:256 * (g + 1):2], ident[:])
+            xg = xgp.tile([P, 1024], BF16, name="xg", align_bytes=64)
+            if m in XCOPY_ON_V:
+                nc.vector.tensor_copy(out=xg[:].bitcast(F32).rearrange("p (g r u) -> p g r u", g=2, u=2),
+                                      in_=xt[:].rearrange("p (g u) r -> p g r u", u=2))
+            else:
+                nc.scalar.copy(out=xg[:].bitcast(F32).rearrange("p (g r u) -> p g r u", g=2, u=2),
+                               in_=xt[:].rearrange("p (g u) r -> p g r u", u=2))
+            nc.vector.quantize_mx(out=xc[:, m, :].bitcast(FP8X4), scales=xs[:, m, :], in_=xg[:])
+
+        wc = []
+        wsc = []
+        for c in range(NCH):
+            wc.append(const.tile([P, 2 * CW], U32, name="wc%d" % c, align_bytes=64))
+            wsc.append(const.tile([P, 2 * CW], U8, name="wsc%d" % c, align_bytes=64))
+        wpl = {}
+        wg = {}
+
+        def widen(c, g, t):
+            if (g, t) == (0, 0):
+                wpl[c] = wplp.tile([P, 2, 4, CW], BF16, name="wpl")
+            src = wb[c][:, g, t, :].bitcast(FP8)
+            col = ws[:, g, t:t + 1]
+            if (c, g) in WIDEN_ON_V:
+                nc.vector.tensor_scalar(out=wpl[c][:, g, t, :], in0=src, scalar1=col, scalar2=None,
+                                        op0=ALU.mult)
+            else:
+                nc.scalar.activation(out=wpl[c][:, g, t, :], in_=src, func=ACT.Copy, scale=col)
+
+        def interleave(c, g):
+            if g == 0:
+                wg[c] = wgp.tile([P, 2, CW, 4], BF16, name="wg", align_bytes=64)
+            dst = wg[c][:, g].rearrange("p (a i) t -> p a t i", i=4)
+            src = wpl[c][:, g].rearrange("p t (a i) -> p a t i", i=4)
+            if (c, g) in S_IL:
+                nc.scalar.copy(out=dst, in_=src)
+            else:
+                nc.vector.tensor_copy(out=dst, in_=src)
+
+        def quant_w(c):
+            nc.vector.quantize_mx(out=wc[c][:].bitcast(FP8X4), scales=wsc[c][:],
+                                  in_=wg[c][:].rearrange("p g n t -> p (g n t)"))
+
+        s_tasks = []
+        v_tasks = []
+        for c in PREP_ORDER:
+            for g in range(2):
+                for t in range(4):
+                    s_tasks.append((c, g, t))
+            v_tasks.append((c, 0))
+            v_tasks.append((c, 1))
+            v_tasks.append((c, 2))
+        s_done = [0]
+        v_done = [0]
+
+        def run_s(n):
+            for k in range(n):
+                if s_done[0] < len(s_tasks):
+                    c, g, t = s_tasks[s_done[0]]
+                    widen(c, g, t)
+                    s_done[0] += 1
+
+        def run_v(n):
+            for k in range(n):
+                if v_done[0] < len(v_tasks):
+                    c, step = v_tasks[v_done[0]]
+                    need = 8 * PREP_ORDER.index(c) + (4 if step == 0 else 8)
+                    run_s(max(0, need - s_done[0]))
+                    if step < 2:
+                        interleave(c, step)
+                    else:
+                        quant_w(c)
+                    v_done[0] += 1
+
+        def ensure(c):
+            run_v(max(0, 3 * (PREP_ORDER.index(c) + 1) - v_done[0]))
+
+        accs = {}
+        ots = {}
+
+        def emit_mm(job):
+            c, b, i = job
+            ensure(c)
+            m = 4 * b + i
+            acc = psa.tile([P, 8, 64], F32, name="acc")
+            accs[job] = acc
+            for g in range(2):
+                nc.tensor.matmul_mx(out=acc[:].rearrange("p h d -> p (h d)"),
+                                    lhsT=xc[:, m, P * g:P * (g + 1)].bitcast(FP8X4),
+                                    lhsT_scale=xs[:, m, P * g:P * (g + 1)],
+                                    rhs=wc[c][:, CW * g:CW * (g + 1)].bitcast(FP8X4),
+                                    rhs_scale=wsc[c][:, CW * g:CW * (g + 1)],
+                                    start=(g == 0), stop=(g == 1))
+
+        def emit_evac(job):
+            c, b, i = job
+            acc = accs[job]
+            if i == 0:
+                ots[(c, b)] = otp.tile([P, 8, 4, 64], F32, name="ot")
+            ot = ots[(c, b)]
+            if c < 4:
+                nd = 64 if PASS_ON_V else 48
+                nc.vector.tensor_tensor(out=ot[:, :, i, 0:nd], in0=acc[:, :, 0:nd],
+                                        in1=ctab[:, i, 0:nd].unsqueeze(1).to_broadcast([P, 8, nd]),
+                                        op=ALU.mult)
+                tb = tbp.tile([P, 8, 24, 2], F32, name="tb")
+                nc.vector.tensor_tensor(
+                    out=tb[:],
+                    in0=acc[:, :, 0:48].rearrange("p h (j e) -> p h j e", e=2)[:, :, :, ::-1],
+                    in1=stab[:, i, 0:48].rearrange("p (j e) -> p j e", e=2).unsqueeze(1)
+                    .to_broadcast([P, 8, 24, 2]),
+                    op=ALU.mult)
+                if not PASS_ON_V:
+                    nc.scalar.copy(out=ot[:, :, i, 48:64], in_=acc[:, :, 48:64])
+                eng = nc.vector if job in V_ADDS else nc.gpsimd
+                eng.tensor_tensor(out=ot[:, :, i, 0:48], in0=ot[:, :, i, 0:48],
+                                  in1=tb[:].rearrange("p h j e -> p h (j e)"), op=ALU.add)
+            else:
+                nc.scalar.copy(out=ot[:, :, i, :], in_=acc[:])
+            which, half = c // 2, c % 2
+            dst = outs[which][b, 8 * half:8 * half + 8].rearrange("h (p i) d -> p h (i d)", i=4)
+            src = ot[:].rearrange("p h i d -> p h (i d)")
+            if (c, b) in SPLIT_UNITS:
+                if i % 2 == 1:
+                    nc.sync.dma_start(out=dst[:, :, 64 * (i - 1):64 * (i + 1)],
+                                      in_=src[:, :, 64 * (i - 1):64 * (i + 1)])
+            elif i == 3:
+                nc.sync.dma_start(out=dst, in_=src)
+
+        run_s(8)
+        for i in range(4):
+            prep_x(0, i)
+        run_v(3)
+        for i in range(4):
+            prep_x(1, i)
+        run_s(8)
+        for k in range(len(jobs) + LOOKAHEAD):
+            if k < len(jobs):
+                emit_mm(jobs[k])
+            if k >= LOOKAHEAD:
+                emit_evac(jobs[k - LOOKAHEAD])
+                run_s(S_PACE)
+                if k % V_PACE == 0:
+                    run_v(1)

@@ -51,7 +51,7 @@ def make_jobs():
     assert nv == 16
     return jobs
 
-S_IL = ((2, 0), (5, 0), (3, 0))
+S_IL = ((2, 0), (5, 0), (3, 0), (3, 1))
 V_ADDS = ((3, 1, 2), (3, 1, 3))
 
 
@@ -119,7 +119,8 @@ def tile_attention_pa_kernel(tc, x, Wqkv_bytes, Wqkv_scale, out_0, out_1, out_2)
         i28 = const.tile([P, 4], F32, name="i28")
         nc.gpsimd.iota(i28[:], pattern=[[28, 4]], base=-210, channel_multiplier=0,
                        allow_small_or_imprecise_dtypes=True)
-        nc.vector.tensor_tensor(out=fq[:, 1, :], in0=fq[:, 0, :], in1=sg[:], op=ALU.mult)
+        nc.vector.scalar_tensor_tensor(out=fq[:, 1, :], in0=fq[:, 0, :], scalar=-1.0, in1=sg[:],
+                                       op0=ALU.mult, op1=ALU.mult)
         idx = const.tile([P, 3], I32, name="idx")
         nc.vector.tensor_scalar(out=idx[:, 0:1], in0=pi[:], scalar1=5, scalar2=None,
                                 op0=ALU.logical_shift_right)
@@ -266,7 +267,10 @@ def tile_attention_pa_kernel(tc, x, Wqkv_bytes, Wqkv_scale, out_0, out_1, out_2)
             c, b, i = job
             ensure(c)
             m = 4 * b + i
-            acc = psa.tile([P, 8, 64], F32, name="acc")
+            if c < 4:
+                acc = psa.tile([P, 8, 64], F32, name="acc")
+            else:
+                acc = psx.tile([P, 8, 64], F32, name="xt")
             accs[job] = acc
             for g in range(2):
                 nc.tensor.matmul_mx(out=acc[:].rearrange("p h d -> p (h d)"),
@@ -289,16 +293,15 @@ def tile_attention_pa_kernel(tc, x, Wqkv_bytes, Wqkv_scale, out_0, out_1, out_2)
                                         op=ALU.mult)
                 tb = tbp.tile([P, 8, 24, 2], F32, name="tb")
                 nc.vector.tensor_tensor(
-                    out=tb[:],
-                    in0=acc[:, :, 0:48].rearrange("p h (j e) -> p h j e", e=2)[:, :, :, ::-1],
-                    in1=stab[:, i, 0:48].rearrange("p (j e) -> p j e", e=2).unsqueeze(1)
-                    .to_broadcast([P, 8, 24, 2]),
+                    out=tb[:].rearrange("p h j e -> p h (j e)"),
+                    in0=acc[:, :, 0:48],
+                    in1=stab[:, i, 0:48].unsqueeze(1).to_broadcast([P, 8, 48]),
                     op=ALU.mult)
                 if not PASS_ON_V:
                     nc.scalar.copy(out=ot[:, :, i, 48:64], in_=acc[:, :, 48:64])
                 eng = nc.vector if job in V_ADDS else nc.gpsimd
-                eng.tensor_tensor(out=ot[:, :, i, 0:48], in0=ot[:, :, i, 0:48],
-                                  in1=tb[:].rearrange("p h j e -> p h (j e)"), op=ALU.add)
+                rot = ot[:, :, i, 0:48].rearrange("p h (j e) -> p h j e", e=2)
+                eng.tensor_tensor(out=rot, in0=rot, in1=tb[:, :, :, ::-1], op=ALU.add)
             else:
                 nc.scalar.copy(out=ot[:, :, i, :], in_=acc[:])
             which, half = c // 2, c % 2

@@ -19,60 +19,35 @@ ACT = mybir.ActivationFunctionType
 P = 128
 NCH = 6
 CW = 512
-LOOKAHEAD = 2
-WIDEN_ON_V = ((0, 1),)
-V_AFTER = (12, 13, 14, 15, 16, 17, 18, 19, 20, 21, 22, 23, 24, 25, 26, 27)
-PASS_ON_V = True
-XCOPY_ON_V = (5,)
-TB_BUFS = 4
-OT_BUFS = 5
-S_PACE = 1
-V_PACE = 2
-SPLIT_UNITS = ((3, 1),)
-
-
-def make_jobs():
-    v_jobs = []
-    for c in (4, 5):
-        for b in range(2):
-            for i in range(4):
-                v_jobs.append((c, b, i))
-    jobs = []
-    n = 0
-    nv = 0
-    for c in range(4):
-        for b in range(2):
-            for i in range(4):
-                jobs.append((c, b, i))
-                if n in V_AFTER:
-                    jobs.append(v_jobs[nv])
-                    nv += 1
-                n += 1
-    assert nv == 16
-    return jobs
-
-S_IL = ((2, 0), (5, 0), (3, 0), (3, 1))
-V_ADDS = ((3, 1, 2), (3, 1, 3))
+Q0, Q1, K0, K1, V0, V1 = range(NCH)
+S_RATE = (3, 2, 2)
+MM_AHEAD = 3
+V_LAG = 1
+S_BANKS = 4
+V_MAX = 1
+X_AHEAD = 3
+IL_ON_V = ((Q1, 0), (Q1, 1))
+S_ORDER = (K0, V0, K1, V1)
+V0_AT = 24
+V0_STEP = 2
+VP_AHEAD = 3
+ADD_STEP = 5
+LAST_SPLIT = ((K1, 1),)
 
 
 def tile_attention_pa_kernel(tc, x, Wqkv_bytes, Wqkv_scale, out_0, out_1, out_2):
     nc = tc.nc
     outs = (out_0, out_1, out_2)
-    jobs = make_jobs()
-    first_use = {}
-    for k in range(len(jobs)):
-        first_use.setdefault(jobs[k][0], k)
-    PREP_ORDER = tuple(sorted(range(NCH), key=lambda c: first_use[c]))
-
     with ExitStack() as ctx:
         const = ctx.enter_context(tc.tile_pool(name="const", bufs=1))
-        xgp = ctx.enter_context(tc.tile_pool(name="xgp", bufs=3))
-        wplp = ctx.enter_context(tc.tile_pool(name="wplp", bufs=3))
-        wgp = ctx.enter_context(tc.tile_pool(name="wgp", bufs=2))
-        otp = ctx.enter_context(tc.tile_pool(name="otp", bufs=OT_BUFS))
-        tbp = ctx.enter_context(tc.tile_pool(name="tbp", bufs=TB_BUFS))
-        psx = ctx.enter_context(tc.psum_pool(name="psx", bufs=2))
-        psa = ctx.enter_context(tc.psum_pool(name="psa", bufs=6))
+        xgp = ctx.enter_context(tc.tile_pool(name="xgp", bufs=8))
+        wplp = ctx.enter_context(tc.tile_pool(name="wplp", bufs=4))
+        wgp = ctx.enter_context(tc.tile_pool(name="wgp", bufs=4))
+        otp = ctx.enter_context(tc.tile_pool(name="otp", bufs=6))
+        tbp = ctx.enter_context(tc.tile_pool(name="tbp", bufs=6))
+        pss = ctx.enter_context(tc.psum_pool(name="pss", bufs=S_BANKS))
+        psv = ctx.enter_context(tc.psum_pool(name="psv", bufs=8 - S_BANKS))
+        ctx.enter_context(tc.manual_schedule())
 
         ws = const.tile([P, 2, 4], F32, name="ws")
         nc.sync.dma_start(out=ws[:], in_=Wqkv_scale.rearrange("(g p t) o -> p g (t o)", p=P, t=4))
@@ -93,20 +68,17 @@ def tile_attention_pa_kernel(tc, x, Wqkv_bytes, Wqkv_scale, out_0, out_1, out_2)
             for h in range(2):
                 nc.sync.dma_start(out=xsb[b][:, 2 * h:2 * h + 2, :], in_=xv[:, 2 * h:2 * h + 2, :])
 
-        load_w(PREP_ORDER[0])
+        load_w(Q0)
         load_x(0)
-        load_w(PREP_ORDER[1])
+        load_w(Q1)
         load_x(1)
-        for c in PREP_ORDER[2:]:
+        for c in S_ORDER:
             load_w(c)
 
         zero = const.tile([P, 8], F32, name="zero")
         nc.vector.memset(zero[:], 0.0)
         warm = const.tile([P, 8], F32, name="warm")
         nc.scalar.activation(out=warm[:], in_=zero[:], func=ACT.Sin)
-
-        ident = const.tile([P, P], F32, name="ident")
-        make_identity(nc, ident[:])
 
         pi = const.tile([P, 1], I32, name="pi")
         nc.gpsimd.iota(pi[:], pattern=[[0, 1]], base=0, channel_multiplier=1)
@@ -119,79 +91,98 @@ def tile_attention_pa_kernel(tc, x, Wqkv_bytes, Wqkv_scale, out_0, out_1, out_2)
         i28 = const.tile([P, 4], F32, name="i28")
         nc.gpsimd.iota(i28[:], pattern=[[28, 4]], base=-210, channel_multiplier=0,
                        allow_small_or_imprecise_dtypes=True)
-        nc.vector.scalar_tensor_tensor(out=fq[:, 1, :], in0=fq[:, 0, :], scalar=-1.0, in1=sg[:],
-                                       op0=ALU.mult, op1=ALU.mult)
+        ident = const.tile([P, P], F32, name="ident")
+        make_identity(nc, ident[:])
+        identb = const.tile([P, P], BF16, name="identb")
+        nc.gpsimd.tensor_copy(out=identb[:], in_=ident[:])
+
         idx = const.tile([P, 3], I32, name="idx")
+        idf = const.tile([P, 3], F32, name="idf")
+        mm = const.tile([P, 6], F32, name="mm")
+        nn = const.tile([P, 2, 6, 16], F32, name="nn")
+        nflat = nn[:].rearrange("p a s d -> p (a s d)")
+        qi = const.tile([P, 192], I32, name="qi")
+        rr = const.tile([P, 192], F32, name="rr")
+        t1 = const.tile([P, 192], F32, name="t1")
+        t2 = const.tile([P, 192], F32, name="t2")
+        t3 = const.tile([P, 192], F32, name="t3")
+        t4 = const.tile([P, 2, 6, 16], F32, name="t4")
+        tabs = []
+        for a in range(2):
+            tab = const.tile([P, 4, 64], F32, name="tab%d" % a)
+            nc.vector.memset(tab[:, :, 48:64], 1.0)
+            tabs.append(tab)
+        ctab, stab = tabs
+
         nc.vector.tensor_scalar(out=idx[:, 0:1], in0=pi[:], scalar1=5, scalar2=None,
                                 op0=ALU.logical_shift_right)
         nc.vector.tensor_scalar(out=idx[:, 1:2], in0=pi[:], scalar1=2, scalar2=7,
                                 op0=ALU.logical_shift_right, op1=ALU.bitwise_and)
         nc.vector.tensor_scalar(out=idx[:, 2:3], in0=pi[:], scalar1=3, scalar2=None,
                                 op0=ALU.bitwise_and)
-        idf = const.tile([P, 3], F32, name="idf")
+        nc.vector.scalar_tensor_tensor(out=fq[:, 1, :], in0=fq[:, 0, :], scalar=-1.0, in1=sg[:],
+                                       op0=ALU.mult, op1=ALU.mult)
         nc.vector.tensor_copy(out=idf[:], in_=idx[:])
-        mm = const.tile([P, 6], F32, name="mm")
         nc.vector.tensor_scalar(out=mm[:, 0:1], in0=idf[:, 0:1], scalar1=140.0, scalar2=-210.0,
                                 op0=ALU.mult, op1=ALU.add)
         nc.vector.tensor_scalar(out=mm[:, 1:2], in0=idf[:, 1:2], scalar1=60.0, scalar2=-210.0,
                                 op0=ALU.mult, op1=ALU.add)
         nc.vector.scalar_tensor_tensor(out=mm[:, 2:6], in0=idf[:, 2:3].to_broadcast([P, 4]),
                                        scalar=112.0, in1=i28[:], op0=ALU.mult, op1=ALU.add)
-        nn = const.tile([P, 2, 6, 16], F32, name="nn")
-        nc.vector.tensor_tensor(out=nn[:],
-                                in0=mm[:].unsqueeze(1).unsqueeze(3).to_broadcast([P, 2, 6, 16]),
-                                in1=fq[:].unsqueeze(2).to_broadcast([P, 2, 6, 16]), op=ALU.mult)
-        nc.vector.tensor_scalar(out=nn[:, 0], in0=nn[:, 0], scalar1=191835.0, scalar2=None, op0=ALU.add)
-        nc.vector.tensor_scalar(out=nn[:, 1], in0=nn[:, 1], scalar1=191100.0, scalar2=None, op0=ALU.add)
-        nflat = nn[:].rearrange("p a s d -> p (a s d)")
-        qi = const.tile([P, 192], I32, name="qi")
-        nc.vector.tensor_scalar(out=qi[:], in0=nflat, scalar1=1.0 / 2940.0, scalar2=None, op0=ALU.mult)
-        rr = const.tile([P, 192], F32, name="rr")
-        nc.vector.scalar_tensor_tensor(out=rr[:], in0=qi[:], scalar=-2940.0, in1=nflat,
-                                       op0=ALU.mult, op1=ALU.add)
-        t1 = const.tile([P, 192], F32, name="t1")
-        nc.vector.tensor_scalar(out=t1[:], in0=rr[:], scalar1=-1.0, scalar2=1470.0,
-                                op0=ALU.mult, op1=ALU.add)
-        t2 = const.tile([P, 192], F32, name="t2")
-        nc.vector.tensor_tensor(out=t2[:], in0=rr[:], in1=t1[:], op=ALU.min)
-        t3 = const.tile([P, 192], F32, name="t3")
-        nc.vector.scalar_tensor_tensor(out=t3[:], in0=t1[:], scalar=-2940.0, in1=t2[:],
-                                       op0=ALU.add, op1=ALU.max)
-        t4 = const.tile([P, 2, 6, 16], F32, name="t4")
-        nc.vector.scalar_tensor_tensor(out=t4[:].rearrange("p a s d -> p (a s d)"), in0=rr[:],
-                                       scalar=-2940.0, in1=t3[:], op0=ALU.add, op1=ALU.max)
-        tabs = []
-        for a in range(2):
-            tab = const.tile([P, 4, 64], F32, name="tab%d" % a)
-            nc.vector.memset(tab[:, :, 48:64], 1.0)
-            nc.scalar.activation(out=tab[:, :, 0:32],
-                                 in_=t4[:, a, 0:2, :].rearrange("p s d -> p (s d)").unsqueeze(1)
-                                 .to_broadcast([P, 4, 32]),
-                                 func=ACT.Sin, scale=math.pi / 1470.0)
-            nc.scalar.activation(out=tab[:, :, 32:48], in_=t4[:, a, 2:6, :],
-                                 func=ACT.Sin, scale=math.pi / 1470.0)
-            tabs.append(tab)
-        ctab, stab = tabs
+
+
+        angle_steps = [
+            lambda: nc.vector.tensor_tensor(
+                out=nn[:], in0=mm[:].unsqueeze(1).unsqueeze(3).to_broadcast([P, 2, 6, 16]),
+                in1=fq[:].unsqueeze(2).to_broadcast([P, 2, 6, 16]), op=ALU.mult),
+            lambda: nc.vector.tensor_scalar(out=nn[:, 0], in0=nn[:, 0], scalar1=191835.0,
+                                            scalar2=None, op0=ALU.add),
+            lambda: nc.vector.tensor_scalar(out=nn[:, 1], in0=nn[:, 1], scalar1=191100.0,
+                                            scalar2=None, op0=ALU.add),
+            lambda: nc.vector.tensor_scalar(out=qi[:], in0=nflat, scalar1=1.0 / 2940.0, scalar2=None,
+                                            op0=ALU.mult),
+            lambda: nc.vector.scalar_tensor_tensor(out=rr[:], in0=qi[:], scalar=-2940.0, in1=nflat,
+                                                   op0=ALU.mult, op1=ALU.add),
+            lambda: nc.vector.tensor_scalar(out=t1[:], in0=rr[:], scalar1=-1.0, scalar2=1470.0,
+                                            op0=ALU.mult, op1=ALU.add),
+            lambda: nc.vector.tensor_tensor(out=t2[:], in0=rr[:], in1=t1[:], op=ALU.min),
+            lambda: nc.vector.scalar_tensor_tensor(out=t3[:], in0=t1[:], scalar=-2940.0, in1=t2[:],
+                                                   op0=ALU.add, op1=ALU.max),
+            lambda: nc.vector.scalar_tensor_tensor(out=t4[:].rearrange("p a s d -> p (a s d)"), in0=rr[:],
+                                                   scalar=-2940.0, in1=t3[:], op0=ALU.add, op1=ALU.max),
+        ]
+
+        def sines():
+            for a in range(2):
+                nc.scalar.activation(out=tabs[a][:, :, 0:32],
+                                     in_=t4[:, a, 0:2, :].rearrange("p s d -> p (s d)").unsqueeze(1)
+                                     .to_broadcast([P, 4, 32]),
+                                     func=ACT.Sin, scale=math.pi / 1470.0)
+                nc.scalar.activation(out=tabs[a][:, :, 32:48], in_=t4[:, a, 2:6, :],
+                                     func=ACT.Sin, scale=math.pi / 1470.0)
 
         xc = const.tile([P, 8, 256], U32, name="xc", align_bytes=64)
         xs = const.tile([P, 8, 256], U8, name="xs", align_bytes=64)
+        xt = {}
+        xg = {}
 
-        def prep_x(b, i):
-            m = 4 * b + i
-            words = xsb[b][:, i, :].bitcast(F32)
-            xt = psx.tile([P, 4, P], F32, name="xt")
+        def x_turn(m):
+            words = xsb[m // 4][:, m % 4, :].bitcast(F32)
+            bank = pss.tile([P, 4, P], F32, name="sbank")
             for g in range(2):
                 for u in range(2):
-                    nc.tensor.transpose(xt[:, 2 * g + u, :],
+                    nc.tensor.transpose(bank[:, 2 * g + u, :],
                                         words[:, 256 * g + u:256 * (g + 1):2], ident[:])
-            xg = xgp.tile([P, 1024], BF16, name="xg", align_bytes=64)
-            if m in XCOPY_ON_V:
-                nc.vector.tensor_copy(out=xg[:].bitcast(F32).rearrange("p (g r u) -> p g r u", g=2, u=2),
-                                      in_=xt[:].rearrange("p (g u) r -> p g r u", u=2))
-            else:
-                nc.scalar.copy(out=xg[:].bitcast(F32).rearrange("p (g r u) -> p g r u", g=2, u=2),
-                               in_=xt[:].rearrange("p (g u) r -> p g r u", u=2))
-            nc.vector.quantize_mx(out=xc[:, m, :].bitcast(FP8X4), scales=xs[:, m, :], in_=xg[:])
+            xt[m] = bank
+
+        def x_copy(m):
+            xg[m] = xgp.tile([P, 1024], BF16, name="xg", align_bytes=64)
+            nc.scalar.copy(out=xg[m][:].bitcast(F32).rearrange("p (g r u) -> p g r u", g=2, u=2),
+                           in_=xt[m][:].rearrange("p (g u) r -> p g r u", u=2))
+
+        def x_quant(m):
+            nc.vector.quantize_mx(out=xc[:, m, :].bitcast(FP8X4), scales=xs[:, m, :], in_=xg[m][:])
+            quanted.add(("x", m))
 
         wc = []
         wsc = []
@@ -200,77 +191,61 @@ def tile_attention_pa_kernel(tc, x, Wqkv_bytes, Wqkv_scale, out_0, out_1, out_2)
             wsc.append(const.tile([P, 2 * CW], U8, name="wsc%d" % c, align_bytes=64))
         wpl = {}
         wg = {}
+        ilb = {}
 
-        def widen(c, g, t):
-            if (g, t) == (0, 0):
-                wpl[c] = wplp.tile([P, 2, 4, CW], BF16, name="wpl")
+        def widen(c, g, t, on_v=False):
+            if (c, g) not in wpl:
+                wpl[(c, g)] = wplp.tile([P, 4, CW], BF16, name="wpl")
             src = wb[c][:, g, t, :].bitcast(FP8)
             col = ws[:, g, t:t + 1]
-            if (c, g) in WIDEN_ON_V:
-                nc.vector.tensor_scalar(out=wpl[c][:, g, t, :], in0=src, scalar1=col, scalar2=None,
+            if on_v:
+                nc.vector.tensor_scalar(out=wpl[(c, g)][:, t, :], in0=src, scalar1=col, scalar2=None,
                                         op0=ALU.mult)
             else:
-                nc.scalar.activation(out=wpl[c][:, g, t, :], in_=src, func=ACT.Copy, scale=col)
+                nc.scalar.activation(out=wpl[(c, g)][:, t, :], in_=src, func=ACT.Copy, scale=col)
 
-        def interleave(c, g):
-            if g == 0:
-                wg[c] = wgp.tile([P, 2, CW, 4], BF16, name="wg", align_bytes=64)
-            dst = wg[c][:, g].rearrange("p (a i) t -> p a t i", i=4)
-            src = wpl[c][:, g].rearrange("p t (a i) -> p a t i", i=4)
-            if (c, g) in S_IL:
-                nc.scalar.copy(out=dst, in_=src)
-            else:
-                nc.vector.tensor_copy(out=dst, in_=src)
+        def il_v(c, g):
+            wg[(c, g)] = wgp.tile([P, CW, 4], BF16, name="wg", align_bytes=64)
+            nc.vector.tensor_copy(out=wg[(c, g)][:].rearrange("p (a i) t -> p a t i", i=4),
+                                  in_=wpl[(c, g)][:].rearrange("p t (a i) -> p a t i", i=4))
 
-        def quant_w(c):
-            nc.vector.quantize_mx(out=wc[c][:].bitcast(FP8X4), scales=wsc[c][:],
-                                  in_=wg[c][:].rearrange("p g n t -> p (g n t)"))
+        def il_pe(c, g, q):
+            bank = pss.tile([P, 256, 4], BF16, name="sbank")
+            for r in range(2):
+                n0 = 256 * q + P * r
+                nc.tensor.matmul(bank[:, P * r:P * (r + 1), :].rearrange("p n t -> p t n"),
+                                 lhsT=identb[:], rhs=wpl[(c, g)][:, :, n0:n0 + P],
+                                 start=True, stop=True)
+            ilb[(c, g, q)] = bank
 
-        s_tasks = []
-        v_tasks = []
-        for c in PREP_ORDER:
-            for g in range(2):
-                for t in range(4):
-                    s_tasks.append((c, g, t))
-            v_tasks.append((c, 0))
-            v_tasks.append((c, 1))
-            v_tasks.append((c, 2))
-        s_done = [0]
-        v_done = [0]
+        def il_copy(c, g, q):
+            if q == 0:
+                wg[(c, g)] = wgp.tile([P, CW, 4], BF16, name="wg", align_bytes=64)
+            nc.scalar.copy(out=wg[(c, g)][:, 256 * q:256 * (q + 1), :], in_=ilb[(c, g, q)][:])
 
-        def run_s(n):
-            for k in range(n):
-                if s_done[0] < len(s_tasks):
-                    c, g, t = s_tasks[s_done[0]]
-                    widen(c, g, t)
-                    s_done[0] += 1
-
-        def run_v(n):
-            for k in range(n):
-                if v_done[0] < len(v_tasks):
-                    c, step = v_tasks[v_done[0]]
-                    need = 8 * PREP_ORDER.index(c) + (4 if step == 0 else 8)
-                    run_s(max(0, need - s_done[0]))
-                    if step < 2:
-                        interleave(c, step)
-                    else:
-                        quant_w(c)
-                    v_done[0] += 1
-
-        def ensure(c):
-            run_v(max(0, 3 * (PREP_ORDER.index(c) + 1) - v_done[0]))
+        def w_quant(c, g):
+            nc.vector.quantize_mx(out=wc[c][:, CW * g:CW * (g + 1)].bitcast(FP8X4),
+                                  scales=wsc[c][:, CW * g:CW * (g + 1)],
+                                  in_=wg[(c, g)][:].rearrange("p n t -> p (n t)"))
+            quanted.add((c, g))
 
         accs = {}
         ots = {}
 
-        def emit_mm(job):
+        quanted = set()
+
+        def product(job):
             c, b, i = job
-            ensure(c)
             m = 4 * b + i
-            if c < 4:
-                acc = psa.tile([P, 8, 64], F32, name="acc")
+            while not {("x", m), (c, 0), (c, 1)} <= quanted:
+                if v_todo:
+                    next_v()
+                else:
+                    s_step(0)
+            if c < V0:
+                acc = psv.tile([P, 8, 64], F32, name="acc")
             else:
-                acc = psx.tile([P, 8, 64], F32, name="xt")
+                acc = pss.tile([P, 8, 64], F32, name="sbank")
             accs[job] = acc
             for g in range(2):
                 nc.tensor.matmul_mx(out=acc[:].rearrange("p h d -> p (h d)"),
@@ -280,52 +255,147 @@ def tile_attention_pa_kernel(tc, x, Wqkv_bytes, Wqkv_scale, out_0, out_1, out_2)
                                     rhs_scale=wsc[c][:, CW * g:CW * (g + 1)],
                                     start=(g == 0), stop=(g == 1))
 
-        def emit_evac(job):
+        def store(job):
             c, b, i = job
-            acc = accs[job]
-            if i == 0:
-                ots[(c, b)] = otp.tile([P, 8, 4, 64], F32, name="ot")
-            ot = ots[(c, b)]
-            if c < 4:
-                nd = 64 if PASS_ON_V else 48
-                nc.vector.tensor_tensor(out=ot[:, :, i, 0:nd], in0=acc[:, :, 0:nd],
-                                        in1=ctab[:, i, 0:nd].unsqueeze(1).to_broadcast([P, 8, nd]),
-                                        op=ALU.mult)
-                tb = tbp.tile([P, 8, 24, 2], F32, name="tb")
-                nc.vector.tensor_tensor(
-                    out=tb[:].rearrange("p h j e -> p h (j e)"),
-                    in0=acc[:, :, 0:48],
-                    in1=stab[:, i, 0:48].unsqueeze(1).to_broadcast([P, 8, 48]),
-                    op=ALU.mult)
-                if not PASS_ON_V:
-                    nc.scalar.copy(out=ot[:, :, i, 48:64], in_=acc[:, :, 48:64])
-                eng = nc.vector if job in V_ADDS else nc.gpsimd
-                rot = ot[:, :, i, 0:48].rearrange("p h (j e) -> p h j e", e=2)
-                eng.tensor_tensor(out=rot, in0=rot, in1=tb[:, :, :, ::-1], op=ALU.add)
-            else:
-                nc.scalar.copy(out=ot[:, :, i, :], in_=acc[:])
             which, half = c // 2, c % 2
             dst = outs[which][b, 8 * half:8 * half + 8].rearrange("h (p i) d -> p h (i d)", i=4)
-            src = ot[:].rearrange("p h i d -> p h (i d)")
-            if (c, b) in SPLIT_UNITS:
+            src = ots[(c, b)][:].rearrange("p h i d -> p h (i d)")
+            if (c, b) in LAST_SPLIT:
                 if i % 2 == 1:
                     nc.sync.dma_start(out=dst[:, :, 64 * (i - 1):64 * (i + 1)],
                                       in_=src[:, :, 64 * (i - 1):64 * (i + 1)])
             elif i == 3:
                 nc.sync.dma_start(out=dst, in_=src)
 
-        run_s(8)
-        for i in range(4):
-            prep_x(0, i)
-        run_v(3)
-        for i in range(4):
-            prep_x(1, i)
-        run_s(8)
-        for k in range(len(jobs) + LOOKAHEAD):
-            if k < len(jobs):
-                emit_mm(jobs[k])
-            if k >= LOOKAHEAD:
-                emit_evac(jobs[k - LOOKAHEAD])
-                run_s(S_PACE)
-                if k % V_PACE == 0:
-                    run_v(1)
+        def out_tile(job):
+            c, b, i = job
+            if i == 0:
+                ots[(c, b)] = otp.tile([P, 8, 4, 64], F32, name="ot")
+            return ots[(c, b)]
+
+        def rotate(job, add_on_v):
+            c, b, i = job
+            acc = accs[job]
+            ot = out_tile(job)
+            nc.vector.tensor_tensor(out=ot[:, :, i, :], in0=acc[:],
+                                    in1=ctab[:, i, :].unsqueeze(1).to_broadcast([P, 8, 64]),
+                                    op=ALU.mult)
+            tb = tbp.tile([P, 8, 24, 2], F32, name="tb")
+            nc.vector.tensor_tensor(out=tb[:].rearrange("p h j e -> p h (j e)"),
+                                    in0=acc[:, :, 0:48],
+                                    in1=stab[:, i, 0:48].unsqueeze(1).to_broadcast([P, 8, 48]),
+                                    op=ALU.mult)
+            eng = nc.vector if add_on_v else nc.gpsimd
+            rot = ot[:, :, i, 0:48].rearrange("p h (j e) -> p h j e", e=2)
+            eng.tensor_tensor(out=rot, in0=rot, in1=tb[:, :, :, ::-1], op=ALU.add)
+            store(job)
+
+        def v_copy(job):
+            c, b, i = job
+            ot = out_tile(job)
+            nc.scalar.copy(out=ot[:, :, i, :], in_=accs[job][:])
+            store(job)
+
+        rots = [(c, b, i) for c in (Q0, Q1, K0, K1) for b in range(2) for i in range(4)]
+
+        halves = [(c, g) for c in S_ORDER for g in range(2)]
+        units = [(x_copy, (m,)) for m in range(4, 8)] + [(widen, (Q1, 1, t)) for t in range(4)]
+        v_ready = []
+        for n in range(len(halves) + 2):
+            for t in range(4):
+                if n < len(halves):
+                    units.append((widen, halves[n] + (t,)))
+                if t == 0 and n > 1:
+                    units.append((il_copy, halves[n - 2] + (1,)))
+                if t == 0 and 0 < n <= len(halves):
+                    units.append((il_pe, halves[n - 1] + (0,)))
+                    units.append((il_pe, halves[n - 1] + (1,)))
+                if t == 3 and 0 < n <= len(halves):
+                    units.append((il_copy, halves[n - 1] + (0,)))
+                if 4 * n + t == V0_AT:
+                    v_ready = [(V0, b, i) for b in range(2) for i in range(4)]
+                if v_ready and (4 * n + t) % V0_STEP == 1:
+                    units.append((v_copy, (v_ready.pop(0),)))
+        for j in v_ready + [(V1, b, i) for b in range(2) for i in range(4)]:
+            units.append((v_copy, (j,)))
+
+        s_at = [0]
+        v_todo = []
+        v_issued = set()
+
+        def s_step(slot):
+            fn, args = units[s_at[0]]
+            for ahead in units[s_at[0]:s_at[0] + VP_AHEAD]:
+                if ahead[0] == v_copy and ahead[1][0] not in v_issued:
+                    v_issued.add(ahead[1][0])
+                    product(ahead[1][0])
+            s_at[0] += 1
+            if fn == il_pe:
+                fn(*args)
+                if s_at[0] < len(units):
+                    s_step(slot)
+                return
+            fn(*args)
+            if fn == widen and args[0] == Q1 and args[2] == 3:
+                v_todo.append((slot, il_v, args[0:2]))
+                v_todo.append((slot + 1, w_quant, args[0:2]))
+            elif fn == il_copy and args[2] == 1:
+                v_todo.append((slot, w_quant, args[0:2]))
+            elif fn == x_copy:
+                v_todo.append((slot, x_quant, args))
+                if args[0] == 5:
+                    v_todo.append((slot, il_v, (Q1, 0)))
+                    v_todo.append((slot + 1, w_quant, (Q1, 0)))
+                if args[0] + X_AHEAD < 8:
+                    x_turn(args[0] + X_AHEAD)
+
+        def next_v():
+            at, fn, args = v_todo.pop(0)
+            fn(*args)
+
+        def angle():
+            if angle_steps:
+                angle_steps.pop(0)()
+
+        for t in range(4):
+            widen(Q0, 0, t)
+        for t in range(4):
+            widen(Q0, 1, t, on_v=True)
+            angle()
+        for m in range(X_AHEAD):
+            x_turn(m)
+        il_v(Q0, 0)
+        angle()
+        il_v(Q0, 1)
+        angle()
+        for m in range(4):
+            x_copy(m)
+            if m + X_AHEAD < 8:
+                x_turn(m + X_AHEAD)
+        for t in range(4):
+            widen(Q1, 0, t)
+        x_quant(0)
+        angle()
+        w_quant(Q0, 0)
+        angle()
+        x_quant(1)
+        angle()
+        w_quant(Q0, 1)
+        x_quant(2)
+        x_quant(3)
+        sines()
+        for k in range(MM_AHEAD):
+            product(rots[k])
+        for k in range(len(rots)):
+            for n in range(S_RATE[k % len(S_RATE)]):
+                if s_at[0] < len(units):
+                    s_step(k)
+            n = 0
+            while v_todo and v_todo[0][0] + V_LAG <= k and n < V_MAX:
+                next_v()
+                n += 1
+            rotate(rots[k], k % ADD_STEP == ADD_STEP - 1 or k >= 30)
+            if k + MM_AHEAD < len(rots):
+                product(rots[k + MM_AHEAD])
+        while s_at[0] < len(units):
+            s_step(len(rots))

@@ -20,18 +20,20 @@ P = 128
 NCH = 6
 CW = 512
 Q0, Q1, K0, K1, V0, V1 = range(NCH)
-S_RATE = (3, 2, 2)
-MM_AHEAD = 3
-V_LAG = 1
+V_STEPS = {V0: (0, 2, 3), Q1: (4, 5, 6), K0: (8, 10, 12), V1: (15,), K1: (21, 22)}
+X_STEPS = (0, 1, 3, 3)
 S_BANKS = 4
-V_MAX = 1
+MM_AHEAD = 3
 X_AHEAD = 3
-IL_ON_V = ((Q1, 0), (Q1, 1))
-S_ORDER = (K0, V0, K1, V1)
-V0_AT = 24
-V0_STEP = 2
-VP_AHEAD = 3
-ADD_STEP = 5
+S_FIRST = 8
+V1_EARLY = 4
+V1_SKIP = 4
+K1_ON_S = (0,)
+V1_STEP = 1
+S_RATE = 2.4
+VM_AT = {V0: 4, V1: 16}
+VM_STEP = 1
+LAST_ADDS = 2
 LAST_SPLIT = ((K1, 1),)
 
 
@@ -41,8 +43,8 @@ def tile_attention_pa_kernel(tc, x, Wqkv_bytes, Wqkv_scale, out_0, out_1, out_2)
     with ExitStack() as ctx:
         const = ctx.enter_context(tc.tile_pool(name="const", bufs=1))
         xgp = ctx.enter_context(tc.tile_pool(name="xgp", bufs=8))
-        wplp = ctx.enter_context(tc.tile_pool(name="wplp", bufs=4))
-        wgp = ctx.enter_context(tc.tile_pool(name="wgp", bufs=4))
+        wplp = ctx.enter_context(tc.tile_pool(name="wplp", bufs=6))
+        wgp = ctx.enter_context(tc.tile_pool(name="wgp", bufs=3))
         otp = ctx.enter_context(tc.tile_pool(name="otp", bufs=6))
         tbp = ctx.enter_context(tc.tile_pool(name="tbp", bufs=6))
         pss = ctx.enter_context(tc.psum_pool(name="pss", bufs=S_BANKS))
@@ -70,9 +72,10 @@ def tile_attention_pa_kernel(tc, x, Wqkv_bytes, Wqkv_scale, out_0, out_1, out_2)
 
         load_w(Q0)
         load_x(0)
-        load_w(Q1)
+        load_w(V0)
         load_x(1)
-        for c in S_ORDER:
+        load_w(Q1)
+        for c in (K0, V1, K1):
             load_w(c)
 
         zero = const.tile([P, 8], F32, name="zero")
@@ -93,8 +96,6 @@ def tile_attention_pa_kernel(tc, x, Wqkv_bytes, Wqkv_scale, out_0, out_1, out_2)
                        allow_small_or_imprecise_dtypes=True)
         ident = const.tile([P, P], F32, name="ident")
         make_identity(nc, ident[:])
-        identb = const.tile([P, P], BF16, name="identb")
-        nc.gpsimd.tensor_copy(out=identb[:], in_=ident[:])
 
         idx = const.tile([P, 3], I32, name="idx")
         idf = const.tile([P, 3], F32, name="idf")
@@ -165,6 +166,7 @@ def tile_attention_pa_kernel(tc, x, Wqkv_bytes, Wqkv_scale, out_0, out_1, out_2)
         xs = const.tile([P, 8, 256], U8, name="xs", align_bytes=64)
         xt = {}
         xg = {}
+        quanted = set()
 
         def x_turn(m):
             words = xsb[m // 4][:, m % 4, :].bitcast(F32)
@@ -191,7 +193,8 @@ def tile_attention_pa_kernel(tc, x, Wqkv_bytes, Wqkv_scale, out_0, out_1, out_2)
             wsc.append(const.tile([P, 2 * CW], U8, name="wsc%d" % c, align_bytes=64))
         wpl = {}
         wg = {}
-        ilb = {}
+        done = set()
+        widened = set()
 
         def widen(c, g, t, on_v=False):
             if (c, g) not in wpl:
@@ -203,45 +206,28 @@ def tile_attention_pa_kernel(tc, x, Wqkv_bytes, Wqkv_scale, out_0, out_1, out_2)
                                         op0=ALU.mult)
             else:
                 nc.scalar.activation(out=wpl[(c, g)][:, t, :], in_=src, func=ACT.Copy, scale=col)
+            widened.add((c, g, t))
 
-        def il_v(c, g):
-            wg[(c, g)] = wgp.tile([P, CW, 4], BF16, name="wg", align_bytes=64)
-            nc.vector.tensor_copy(out=wg[(c, g)][:].rearrange("p (a i) t -> p a t i", i=4),
-                                  in_=wpl[(c, g)][:].rearrange("p t (a i) -> p a t i", i=4))
+        def interleave(c, g, on_v):
+            if g == 0:
+                wg[c] = wgp.tile([P, 2, CW, 4], BF16, name="wg", align_bytes=64)
+            copy = nc.vector.tensor_copy if on_v else nc.scalar.copy
+            copy(out=wg[c][:, g].rearrange("p (a i) t -> p a t i", i=4),
+                 in_=wpl[(c, g)][:].rearrange("p t (a i) -> p a t i", i=4))
+            done.add((c, g))
 
-        def il_pe(c, g, q):
-            bank = pss.tile([P, 256, 4], BF16, name="sbank")
-            for r in range(2):
-                n0 = 256 * q + P * r
-                nc.tensor.matmul(bank[:, P * r:P * (r + 1), :].rearrange("p n t -> p t n"),
-                                 lhsT=identb[:], rhs=wpl[(c, g)][:, :, n0:n0 + P],
-                                 start=True, stop=True)
-            ilb[(c, g, q)] = bank
-
-        def il_copy(c, g, q):
-            if q == 0:
-                wg[(c, g)] = wgp.tile([P, CW, 4], BF16, name="wg", align_bytes=64)
-            nc.scalar.copy(out=wg[(c, g)][:, 256 * q:256 * (q + 1), :], in_=ilb[(c, g, q)][:])
-
-        def w_quant(c, g):
-            nc.vector.quantize_mx(out=wc[c][:, CW * g:CW * (g + 1)].bitcast(FP8X4),
-                                  scales=wsc[c][:, CW * g:CW * (g + 1)],
-                                  in_=wg[(c, g)][:].rearrange("p n t -> p (n t)"))
-            quanted.add((c, g))
+        def w_quant(c):
+            nc.vector.quantize_mx(out=wc[c][:].bitcast(FP8X4), scales=wsc[c][:],
+                                  in_=wg[c][:].rearrange("p g n t -> p (g n t)"))
+            quanted.add(c)
 
         accs = {}
         ots = {}
 
-        quanted = set()
-
         def product(job):
             c, b, i = job
             m = 4 * b + i
-            while not {("x", m), (c, 0), (c, 1)} <= quanted:
-                if v_todo:
-                    next_v()
-                else:
-                    s_step(0)
+            assert {("x", m), c} <= quanted
             if c < V0:
                 acc = psv.tile([P, 8, 64], F32, name="acc")
             else:
@@ -298,60 +284,50 @@ def tile_attention_pa_kernel(tc, x, Wqkv_bytes, Wqkv_scale, out_0, out_1, out_2)
 
         rots = [(c, b, i) for c in (Q0, Q1, K0, K1) for b in range(2) for i in range(4)]
 
-        halves = [(c, g) for c in S_ORDER for g in range(2)]
-        units = [(x_copy, (m,)) for m in range(4, 8)] + [(widen, (Q1, 1, t)) for t in range(4)]
-        v_ready = []
-        for n in range(len(halves) + 2):
-            for t in range(4):
-                if n < len(halves):
-                    units.append((widen, halves[n] + (t,)))
-                if t == 0 and n > 1:
-                    units.append((il_copy, halves[n - 2] + (1,)))
-                if t == 0 and 0 < n <= len(halves):
-                    units.append((il_pe, halves[n - 1] + (0,)))
-                    units.append((il_pe, halves[n - 1] + (1,)))
-                if t == 3 and 0 < n <= len(halves):
-                    units.append((il_copy, halves[n - 1] + (0,)))
-                if 4 * n + t == V0_AT:
-                    v_ready = [(V0, b, i) for b in range(2) for i in range(4)]
-                if v_ready and (4 * n + t) % V0_STEP == 1:
-                    units.append((v_copy, (v_ready.pop(0),)))
-        for j in v_ready + [(V1, b, i) for b in range(2) for i in range(4)]:
-            units.append((v_copy, (j,)))
+        def widens(c):
+            return [(widen, (c, g, t)) for g in range(2) for t in range(4)]
 
+        def v_jobs(c):
+            return [(c, b, i) for b in range(2) for i in range(4)]
+
+        def woven(a, b, step):
+            out = []
+            b = list(b)
+            for k in range(len(a)):
+                out.append(a[k])
+                if k % step == step - 1 and b:
+                    out.append(b.pop(0))
+            return out + b
+
+        units = woven(widens(V0)[4:] + widens(Q1), [(x_copy, (m,)) for m in range(4, 8)], 2)
+        units += widens(K0)
+        units += woven(widens(V1), [(v_copy, (j,)) for j in v_jobs(V0)], 1)
+        units += [(interleave, (V1, g, False)) for g in range(2)]
+        units += widens(K1)[:V1_SKIP]
+        units += woven(widens(K1)[V1_SKIP:], [(v_copy, (j,)) for j in v_jobs(V1)[:V1_EARLY]], V1_STEP)
+        units += [(interleave, (K1, g, False)) for g in range(2) if g < len(K1_ON_S)]
+        units += [(v_copy, (j,)) for j in v_jobs(V1)[V1_EARLY:]]
         s_at = [0]
-        v_todo = []
-        v_issued = set()
+        spent = [0.0]
 
-        def s_step(slot):
+        def ready(fn, args):
+            if fn == v_copy:
+                return args[0] in accs
+            return True
+
+        def s_step():
             fn, args = units[s_at[0]]
-            for ahead in units[s_at[0]:s_at[0] + VP_AHEAD]:
-                if ahead[0] == v_copy and ahead[1][0] not in v_issued:
-                    v_issued.add(ahead[1][0])
-                    product(ahead[1][0])
+            if fn == v_copy and args[0] not in accs:
+                product(args[0])
             s_at[0] += 1
-            if fn == il_pe:
-                fn(*args)
-                if s_at[0] < len(units):
-                    s_step(slot)
-                return
             fn(*args)
-            if fn == widen and args[0] == Q1 and args[2] == 3:
-                v_todo.append((slot, il_v, args[0:2]))
-                v_todo.append((slot + 1, w_quant, args[0:2]))
-            elif fn == il_copy and args[2] == 1:
-                v_todo.append((slot, w_quant, args[0:2]))
-            elif fn == x_copy:
-                v_todo.append((slot, x_quant, args))
-                if args[0] == 5:
-                    v_todo.append((slot, il_v, (Q1, 0)))
-                    v_todo.append((slot + 1, w_quant, (Q1, 0)))
-                if args[0] + X_AHEAD < 8:
-                    x_turn(args[0] + X_AHEAD)
+            spent[0] += 4.5 if fn == interleave else 1.0
+            if fn == x_copy and args[0] + X_AHEAD < 8:
+                x_turn(args[0] + X_AHEAD)
 
-        def next_v():
-            at, fn, args = v_todo.pop(0)
-            fn(*args)
+        def s_until(target):
+            while target not in done:
+                s_step()
 
         def angle():
             if angle_steps:
@@ -364,38 +340,69 @@ def tile_attention_pa_kernel(tc, x, Wqkv_bytes, Wqkv_scale, out_0, out_1, out_2)
             angle()
         for m in range(X_AHEAD):
             x_turn(m)
-        il_v(Q0, 0)
+        interleave(Q0, 0, True)
         angle()
-        il_v(Q0, 1)
+        interleave(Q0, 1, True)
         angle()
         for m in range(4):
             x_copy(m)
-            if m + X_AHEAD < 8:
-                x_turn(m + X_AHEAD)
+            x_turn(m + X_AHEAD)
         for t in range(4):
-            widen(Q1, 0, t)
+            widen(V0, 0, t)
         x_quant(0)
-        angle()
-        w_quant(Q0, 0)
         angle()
         x_quant(1)
         angle()
-        w_quant(Q0, 1)
+        w_quant(Q0)
+        while angle_steps:
+            angle()
+        sines()
         x_quant(2)
         x_quant(3)
-        sines()
-        for k in range(MM_AHEAD):
-            product(rots[k])
+        issued = [0]
+
+        def issue(upto):
+            while issued[0] < min(upto, len(rots)):
+                c, b, i = rots[issued[0]]
+                if not {("x", 4 * b + i), c} <= quanted:
+                    return
+                product(rots[issued[0]])
+                issued[0] += 1
+
+        issue(MM_AHEAD)
+        v_products = {}
+        for c in (V0, V1):
+            for n in range(8):
+                v_products.setdefault(VM_AT[c] + VM_STEP * n, []).append(v_jobs(c)[n])
         for k in range(len(rots)):
-            for n in range(S_RATE[k % len(S_RATE)]):
-                if s_at[0] < len(units):
-                    s_step(k)
-            n = 0
-            while v_todo and v_todo[0][0] + V_LAG <= k and n < V_MAX:
-                next_v()
-                n += 1
-            rotate(rots[k], k % ADD_STEP == ADD_STEP - 1 or k >= 30)
-            if k + MM_AHEAD < len(rots):
-                product(rots[k + MM_AHEAD])
+            while s_at[0] < len(units) and spent[0] < S_FIRST + S_RATE * k and ready(*units[s_at[0]]):
+                s_step()
+            if k == 0:
+                interleave(V0, 0, True)
+            rotate(rots[k], k >= len(rots) - LAST_ADDS)
+            for n in range(4):
+                if X_STEPS[n] == k:
+                    while 4 + n not in xg:
+                        s_step()
+                    x_quant(4 + n)
+            for c in (V0, Q1, K0, V1, K1):
+                steps = V_STEPS[c]
+                for n in range(len(steps)):
+                    if steps[n] == k:
+                        g = n - len(steps) + 3
+                        if g < 2 and not (c == V0 and g == 0):
+                            while (c, g, 3) not in widened:
+                                s_step()
+                            if g == 1:
+                                s_until((c, 0))
+                            interleave(c, g, True)
+                        elif g == 2:
+                            if len(steps) == 1:
+                                s_until((c, 1))
+                            w_quant(c)
+            for j in v_products.get(k, []):
+                if j not in accs:
+                    product(j)
+            issue(k + 1 + MM_AHEAD)
         while s_at[0] < len(units):
-            s_step(len(rots))
+            s_step()

@@ -20,20 +20,23 @@ P = 128
 NCH = 6
 CW = 512
 Q0, Q1, K0, K1, V0, V1 = range(NCH)
-V_STEPS = {V0: (0, 2, 3), Q1: (4, 5, 6), K0: (8, 10, 12), V1: (15,), K1: (21, 22)}
-X_STEPS = (0, 1, 3, 3)
+V_STEPS = {V0: (1, 3, 4), Q1: (4, 5, 6), K0: (8, 10, 12), V1: (12, 13, 14), K1: (20, 21)}
+X_STEPS = (0, 1, 2, 3, 4, 5)
 S_BANKS = 4
 MM_AHEAD = 3
 X_AHEAD = 3
 S_FIRST = 8
 V1_EARLY = 4
+IL_ON_S = ((K1, 0),)
+V0_EARLY = 0
+V0_STEP = 1
+EARLY_ANGLES = 5
 V1_SKIP = 4
-K1_ON_S = (0,)
 V1_STEP = 1
 S_RATE = 2.4
-VM_AT = {V0: 4, V1: 16}
+VM_AT = {V0: 4, V1: 15}
 VM_STEP = 1
-LAST_ADDS = 2
+LAST_ADDS = 1
 LAST_SPLIT = ((K1, 1),)
 
 
@@ -300,12 +303,13 @@ def tile_attention_pa_kernel(tc, x, Wqkv_bytes, Wqkv_scale, out_0, out_1, out_2)
             return out + b
 
         units = woven(widens(V0)[4:] + widens(Q1), [(x_copy, (m,)) for m in range(4, 8)], 2)
-        units += widens(K0)
-        units += woven(widens(V1), [(v_copy, (j,)) for j in v_jobs(V0)], 1)
-        units += [(interleave, (V1, g, False)) for g in range(2)]
+        units += woven(widens(K0), [(v_copy, (j,)) for j in v_jobs(V0)[:V0_EARLY]], V0_STEP)
+        units += [(interleave, (K0, g, False)) for g in range(2) if (K0, g) in IL_ON_S]
+        units += woven(widens(V1), [(v_copy, (j,)) for j in v_jobs(V0)[V0_EARLY:]], V0_STEP)
+        units += [(interleave, (V1, g, False)) for g in range(2) if (V1, g) in IL_ON_S]
         units += widens(K1)[:V1_SKIP]
         units += woven(widens(K1)[V1_SKIP:], [(v_copy, (j,)) for j in v_jobs(V1)[:V1_EARLY]], V1_STEP)
-        units += [(interleave, (K1, g, False)) for g in range(2) if g < len(K1_ON_S)]
+        units += [(interleave, (K1, g, False)) for g in range(2) if (K1, g) in IL_ON_S]
         units += [(v_copy, (j,)) for j in v_jobs(V1)[V1_EARLY:]]
         s_at = [0]
         spent = [0.0]
@@ -327,38 +331,37 @@ def tile_attention_pa_kernel(tc, x, Wqkv_bytes, Wqkv_scale, out_0, out_1, out_2)
 
         def s_until(target):
             while target not in done:
+                assert target in IL_ON_S
                 s_step()
 
         def angle():
             if angle_steps:
                 angle_steps.pop(0)()
 
-        for t in range(4):
-            widen(Q0, 0, t)
-        for t in range(4):
-            widen(Q0, 1, t, on_v=True)
+        for n in range(EARLY_ANGLES):
             angle()
+        for g in range(2):
+            for t in range(2):
+                widen(Q0, g, t)
+                widen(Q0, g, 2 + t, on_v=True)
+                angle()
         for m in range(X_AHEAD):
             x_turn(m)
         interleave(Q0, 0, True)
         angle()
         interleave(Q0, 1, True)
-        angle()
+        while angle_steps:
+            angle()
         for m in range(4):
             x_copy(m)
-            x_turn(m + X_AHEAD)
+            if m + X_AHEAD < 4:
+                x_turn(m + X_AHEAD)
+        sines()
         for t in range(4):
             widen(V0, 0, t)
         x_quant(0)
-        angle()
-        x_quant(1)
-        angle()
         w_quant(Q0)
-        while angle_steps:
-            angle()
-        sines()
-        x_quant(2)
-        x_quant(3)
+        x_quant(1)
         issued = [0]
 
         def issue(upto):
@@ -369,7 +372,9 @@ def tile_attention_pa_kernel(tc, x, Wqkv_bytes, Wqkv_scale, out_0, out_1, out_2)
                 product(rots[issued[0]])
                 issued[0] += 1
 
-        issue(MM_AHEAD)
+        issue(2)
+        for m in range(4, 4 + X_AHEAD):
+            x_turn(m)
         v_products = {}
         for c in (V0, V1):
             for n in range(8):
@@ -377,28 +382,27 @@ def tile_attention_pa_kernel(tc, x, Wqkv_bytes, Wqkv_scale, out_0, out_1, out_2)
         for k in range(len(rots)):
             while s_at[0] < len(units) and spent[0] < S_FIRST + S_RATE * k and ready(*units[s_at[0]]):
                 s_step()
-            if k == 0:
-                interleave(V0, 0, True)
             rotate(rots[k], k >= len(rots) - LAST_ADDS)
-            for n in range(4):
-                if X_STEPS[n] == k:
-                    while 4 + n not in xg:
+            for m in range(2, 8):
+                if X_STEPS[m - 2] == k:
+                    while m not in xg:
                         s_step()
-                    x_quant(4 + n)
+                    x_quant(m)
             for c in (V0, Q1, K0, V1, K1):
                 steps = V_STEPS[c]
                 for n in range(len(steps)):
                     if steps[n] == k:
-                        g = n - len(steps) + 3
-                        if g < 2 and not (c == V0 and g == 0):
+                        mine = [g for g in range(2) if (c, g) not in IL_ON_S]
+                        if n < len(mine):
+                            g = mine[n]
                             while (c, g, 3) not in widened:
                                 s_step()
-                            if g == 1:
+                            if g == 1 and (c, 0) in IL_ON_S:
                                 s_until((c, 0))
                             interleave(c, g, True)
-                        elif g == 2:
-                            if len(steps) == 1:
-                                s_until((c, 1))
+                        else:
+                            for g in range(2):
+                                s_until((c, g))
                             w_quant(c)
             for j in v_products.get(k, []):
                 if j not in accs:

@@ -20,21 +20,21 @@ P = 128
 NCH = 6
 CW = 512
 Q0, Q1, K0, K1, V0, V1 = range(NCH)
-V_STEPS = {V0: (1, 3, 4), Q1: (4, 5, 6), K0: (8, 10, 12), V1: (12, 13, 14), K1: (20, 21)}
+V_STEPS = {V0: (1, 3, 4), Q1: (4, 5, 6), K0: (8, 10, 12), V1: (15,), K1: (21, 22)}
 X_STEPS = (0, 1, 2, 3, 4, 5)
 S_BANKS = 4
 MM_AHEAD = 3
 X_AHEAD = 3
 S_FIRST = 8
 V1_EARLY = 4
-IL_ON_S = ((K1, 0),)
+IL_ON_S = ((V1, 0), (V1, 1), (K1, 0))
 V0_EARLY = 0
 V0_STEP = 1
 EARLY_ANGLES = 5
 V1_SKIP = 4
 V1_STEP = 1
 S_RATE = 2.4
-VM_AT = {V0: 4, V1: 15}
+VM_AT = {V0: 4, V1: 16}
 VM_STEP = 1
 LAST_ADDS = 1
 LAST_SPLIT = ((K1, 1),)
@@ -55,7 +55,7 @@ def tile_attention_pa_kernel(tc, x, Wqkv_bytes, Wqkv_scale, out_0, out_1, out_2)
         ctx.enter_context(tc.manual_schedule())
 
         ws = const.tile([P, 2, 4], F32, name="ws")
-        nc.sync.dma_start(out=ws[:], in_=Wqkv_scale.rearrange("(g p t) o -> p g (t o)", p=P, t=4))
+        nc.scalar.dma_start(out=ws[:], in_=Wqkv_scale.rearrange("(g p t) o -> p g (t o)", p=P, t=4))
         wview = Wqkv_bytes.rearrange("(g p t) n -> g p t n", p=P, t=4)
         wb = []
         for c in range(NCH):
@@ -258,7 +258,7 @@ def tile_attention_pa_kernel(tc, x, Wqkv_bytes, Wqkv_scale, out_0, out_1, out_2)
 
         def out_tile(job):
             c, b, i = job
-            if i == 0:
+            if (c, b) not in ots:
                 ots[(c, b)] = otp.tile([P, 8, 4, 64], F32, name="ot")
             return ots[(c, b)]
 

@@ -31,11 +31,13 @@ IL_ON_S = ((V1, 0), (V1, 1), (K1, 0))
 V0_EARLY = 0
 V0_STEP = 1
 EARLY_ANGLES = 5
+WARM_UP = 8
 V1_SKIP = 4
 V1_STEP = 1
 S_RATE = 2.4
 VM_AT = {V0: 4, V1: 16}
-VM_STEP = 1
+VM_LAST = 21
+V_ADDS = ()
 LAST_ADDS = 1
 LAST_SPLIT = ((K1, 1),)
 
@@ -83,6 +85,8 @@ def tile_attention_pa_kernel(tc, x, Wqkv_bytes, Wqkv_scale, out_0, out_1, out_2)
 
         zero = const.tile([P, 8], F32, name="zero")
         nc.vector.memset(zero[:], 0.0)
+        blank = const.tile([P, CW], BF16, name="blank")
+        nc.vector.memset(blank[:], 0.0)
         warm = const.tile([P, 8], F32, name="warm")
         nc.scalar.activation(out=warm[:], in_=zero[:], func=ACT.Sin)
 
@@ -303,6 +307,7 @@ def tile_attention_pa_kernel(tc, x, Wqkv_bytes, Wqkv_scale, out_0, out_1, out_2)
             return out + b
 
         units = woven(widens(V0)[4:] + widens(Q1), [(x_copy, (m,)) for m in range(4, 8)], 2)
+        units += [(interleave, (V0, g, False)) for g in range(2) if (V0, g) in IL_ON_S]
         units += woven(widens(K0), [(v_copy, (j,)) for j in v_jobs(V0)[:V0_EARLY]], V0_STEP)
         units += [(interleave, (K0, g, False)) for g in range(2) if (K0, g) in IL_ON_S]
         units += woven(widens(V1), [(v_copy, (j,)) for j in v_jobs(V0)[V0_EARLY:]], V0_STEP)
@@ -338,6 +343,9 @@ def tile_attention_pa_kernel(tc, x, Wqkv_bytes, Wqkv_scale, out_0, out_1, out_2)
             if angle_steps:
                 angle_steps.pop(0)()
 
+        dull = pss.tile([P, CW], F32, name="sbank")
+        for n in range(WARM_UP):
+            nc.tensor.matmul(dull[:], lhsT=blank[:, 0:P], rhs=blank[:], start=True, stop=True)
         for n in range(EARLY_ANGLES):
             angle()
         for g in range(2):
@@ -378,11 +386,11 @@ def tile_attention_pa_kernel(tc, x, Wqkv_bytes, Wqkv_scale, out_0, out_1, out_2)
         v_products = {}
         for c in (V0, V1):
             for n in range(8):
-                v_products.setdefault(VM_AT[c] + VM_STEP * n, []).append(v_jobs(c)[n])
+                v_products.setdefault(min(VM_AT[c] + n, VM_LAST), []).append(v_jobs(c)[n])
         for k in range(len(rots)):
             while s_at[0] < len(units) and spent[0] < S_FIRST + S_RATE * k and ready(*units[s_at[0]]):
                 s_step()
-            rotate(rots[k], k >= len(rots) - LAST_ADDS)
+            rotate(rots[k], k >= len(rots) - LAST_ADDS or k in V_ADDS)
             for m in range(2, 8):
                 if X_STEPS[m - 2] == k:
                     while m not in xg:

@@ -31,7 +31,6 @@ IL_ON_S = ((V1, 0), (V1, 1), (K1, 0))
 V0_EARLY = 0
 V0_STEP = 1
 EARLY_ANGLES = 5
-WARM_UP = 8
 V1_SKIP = 4
 V1_STEP = 1
 S_RATE = 2.4
@@ -85,8 +84,6 @@ def tile_attention_pa_kernel(tc, x, Wqkv_bytes, Wqkv_scale, out_0, out_1, out_2)
 
         zero = const.tile([P, 8], F32, name="zero")
         nc.vector.memset(zero[:], 0.0)
-        blank = const.tile([P, CW], BF16, name="blank")
-        nc.vector.memset(blank[:], 0.0)
         warm = const.tile([P, 8], F32, name="warm")
         nc.scalar.activation(out=warm[:], in_=zero[:], func=ACT.Sin)
 
@@ -112,9 +109,7 @@ def tile_attention_pa_kernel(tc, x, Wqkv_bytes, Wqkv_scale, out_0, out_1, out_2)
         qi = const.tile([P, 192], I32, name="qi")
         rr = const.tile([P, 192], F32, name="rr")
         t1 = const.tile([P, 192], F32, name="t1")
-        t2 = const.tile([P, 192], F32, name="t2")
-        t3 = const.tile([P, 192], F32, name="t3")
-        t4 = const.tile([P, 2, 6, 16], F32, name="t4")
+        t2 = const.tile([P, 2, 6, 16], F32, name="t2")
         tabs = []
         for a in range(2):
             tab = const.tile([P, 4, 64], F32, name="tab%d" % a)
@@ -151,23 +146,19 @@ def tile_attention_pa_kernel(tc, x, Wqkv_bytes, Wqkv_scale, out_0, out_1, out_2)
                                             op0=ALU.mult),
             lambda: nc.vector.scalar_tensor_tensor(out=rr[:], in0=qi[:], scalar=-2940.0, in1=nflat,
                                                    op0=ALU.mult, op1=ALU.add),
-            lambda: nc.vector.tensor_scalar(out=t1[:], in0=rr[:], scalar1=-1.0, scalar2=1470.0,
-                                            op0=ALU.mult, op1=ALU.add),
-            lambda: nc.vector.tensor_tensor(out=t2[:], in0=rr[:], in1=t1[:], op=ALU.min),
-            lambda: nc.vector.scalar_tensor_tensor(out=t3[:], in0=t1[:], scalar=-2940.0, in1=t2[:],
-                                                   op0=ALU.add, op1=ALU.max),
-            lambda: nc.vector.scalar_tensor_tensor(out=t4[:].rearrange("p a s d -> p (a s d)"), in0=rr[:],
-                                                   scalar=-2940.0, in1=t3[:], op0=ALU.add, op1=ALU.max),
         ]
 
         def sines():
+            nc.scalar.activation(out=t1[:], in_=rr[:], func=ACT.Abs, bias=-735.0)
+            nc.scalar.activation(out=t2[:].rearrange("p a s d -> p (a s d)"), in_=t1[:], func=ACT.Abs,
+                                 scale=-1.0, bias=1470.0)
             for a in range(2):
                 nc.scalar.activation(out=tabs[a][:, :, 0:32],
-                                     in_=t4[:, a, 0:2, :].rearrange("p s d -> p (s d)").unsqueeze(1)
+                                     in_=t2[:, a, 0:2, :].rearrange("p s d -> p (s d)").unsqueeze(1)
                                      .to_broadcast([P, 4, 32]),
-                                     func=ACT.Sin, scale=math.pi / 1470.0)
-                nc.scalar.activation(out=tabs[a][:, :, 32:48], in_=t4[:, a, 2:6, :],
-                                     func=ACT.Sin, scale=math.pi / 1470.0)
+                                     func=ACT.Sin, scale=math.pi / 1470.0, bias=-math.pi / 2)
+                nc.scalar.activation(out=tabs[a][:, :, 32:48], in_=t2[:, a, 2:6, :],
+                                     func=ACT.Sin, scale=math.pi / 1470.0, bias=-math.pi / 2)
 
         xc = const.tile([P, 8, 256], U32, name="xc", align_bytes=64)
         xs = const.tile([P, 8, 256], U8, name="xs", align_bytes=64)
@@ -343,9 +334,6 @@ def tile_attention_pa_kernel(tc, x, Wqkv_bytes, Wqkv_scale, out_0, out_1, out_2)
             if angle_steps:
                 angle_steps.pop(0)()
 
-        dull = pss.tile([P, CW], F32, name="sbank")
-        for n in range(WARM_UP):
-            nc.tensor.matmul(dull[:], lhsT=blank[:, 0:P], rhs=blank[:], start=True, stop=True)
         for n in range(EARLY_ANGLES):
             angle()
         for g in range(2):

@@ -21,11 +21,14 @@ NCH = 6
 CW = 512
 Q0, Q1, K0, K1, V0, V1 = range(NCH)
 V_STEPS = {V0: (1, 3, 4), Q1: (4, 5, 6), K0: (8, 10, 12), V1: (15,), K1: (21, 22)}
-X_STEPS = (0, 1, 2, 3, 4, 5)
+X_STEPS = (0, 2, 3, 4, 5)
 S_BANKS = 4
 MM_AHEAD = 3
 X_AHEAD = 3
 S_FIRST = 8
+PASS_FROM = 25
+PASS_TO = 32
+PASS_LEAD = 1
 V1_EARLY = 4
 IL_ON_S = ((V1, 0), (V1, 1), (K1, 0))
 V0_EARLY = 0
@@ -261,8 +264,9 @@ def tile_attention_pa_kernel(tc, x, Wqkv_bytes, Wqkv_scale, out_0, out_1, out_2)
             c, b, i = job
             acc = accs[job]
             ot = out_tile(job)
-            nc.vector.tensor_tensor(out=ot[:, :, i, :], in0=acc[:],
-                                    in1=ctab[:, i, :].unsqueeze(1).to_broadcast([P, 8, 64]),
+            nd = 48 if job in passed else 64
+            nc.vector.tensor_tensor(out=ot[:, :, i, 0:nd], in0=acc[:, :, 0:nd],
+                                    in1=ctab[:, i, 0:nd].unsqueeze(1).to_broadcast([P, 8, nd]),
                                     op=ALU.mult)
             tb = tbp.tile([P, 8, 24, 2], F32, name="tb")
             nc.vector.tensor_tensor(out=tb[:].rearrange("p h j e -> p h (j e)"),
@@ -273,6 +277,13 @@ def tile_attention_pa_kernel(tc, x, Wqkv_bytes, Wqkv_scale, out_0, out_1, out_2)
             rot = ot[:, :, i, 0:48].rearrange("p h (j e) -> p h j e", e=2)
             eng.tensor_tensor(out=rot, in0=rot, in1=tb[:, :, :, ::-1], op=ALU.add)
             store(job)
+
+        passed = set()
+
+        def pass_copy(job):
+            c, b, i = job
+            nc.scalar.copy(out=out_tile(job)[:, :, i, 48:64], in_=accs[job][:, :, 48:64])
+            passed.add(job)
 
         def v_copy(job):
             c, b, i = job
@@ -357,7 +368,8 @@ def tile_attention_pa_kernel(tc, x, Wqkv_bytes, Wqkv_scale, out_0, out_1, out_2)
             widen(V0, 0, t)
         x_quant(0)
         w_quant(Q0)
-        x_quant(1)
+        for m in range(1, 3):
+            x_quant(m)
         issued = [0]
 
         def issue(upto):
@@ -378,9 +390,12 @@ def tile_attention_pa_kernel(tc, x, Wqkv_bytes, Wqkv_scale, out_0, out_1, out_2)
         for k in range(len(rots)):
             while s_at[0] < len(units) and spent[0] < S_FIRST + S_RATE * k and ready(*units[s_at[0]]):
                 s_step()
+            p = k + PASS_LEAD
+            if PASS_FROM <= p < min(PASS_TO, issued[0]):
+                pass_copy(rots[p])
             rotate(rots[k], k >= len(rots) - LAST_ADDS or k in V_ADDS)
-            for m in range(2, 8):
-                if X_STEPS[m - 2] == k:
+            for m in range(3, 8):
+                if X_STEPS[m - 3] == k:
                     while m not in xg:
                         s_step()
                     x_quant(m)

@@ -126,7 +126,7 @@ def tile_attention_pa_kernel(tc, x, Wqkv_bytes, Wqkv_scale, out_0, out_1, out_2)
                                 op0=ALU.logical_shift_right, op1=ALU.bitwise_and)
         nc.vector.tensor_scalar(out=idx[:, 2:3], in0=pi[:], scalar1=3, scalar2=None,
                                 op0=ALU.bitwise_and)
-        nc.vector.scalar_tensor_tensor(out=fq[:, 1, :], in0=fq[:, 0, :], scalar=-1.0, in1=sg[:],
+        nc.vector.scalar_tensor_tensor(out=fq[:, 1, :], in0=fq[:, 0, :], scalar=1.0, in1=sg[:],
                                        op0=ALU.mult, op1=ALU.mult)
         nc.vector.tensor_copy(out=idf[:], in_=idx[:])
         nc.vector.tensor_scalar(out=mm[:, 0:1], in0=idf[:, 0:1], scalar1=140.0, scalar2=-210.0,
@@ -268,14 +268,15 @@ def tile_attention_pa_kernel(tc, x, Wqkv_bytes, Wqkv_scale, out_0, out_1, out_2)
             nc.vector.tensor_tensor(out=ot[:, :, i, 0:nd], in0=acc[:, :, 0:nd],
                                     in1=ctab[:, i, 0:nd].unsqueeze(1).to_broadcast([P, 8, nd]),
                                     op=ALU.mult)
-            tb = tbp.tile([P, 8, 24, 2], F32, name="tb")
-            nc.vector.tensor_tensor(out=tb[:].rearrange("p h j e -> p h (j e)"),
-                                    in0=acc[:, :, 0:48],
-                                    in1=stab[:, i, 0:48].unsqueeze(1).to_broadcast([P, 8, 48]),
-                                    op=ALU.mult)
+            tb = tbp.tile([P, 8, 48], F32, name="tb")
+            nc.vector.tensor_tensor(
+                out=tb[:].rearrange("p h (j e) -> p h j e", e=2),
+                in0=acc[:, :, 0:48].rearrange("p h (j e) -> p h j e", e=2)[:, :, :, ::-1],
+                in1=stab[:, i, 0:48].rearrange("p (j e) -> p j e", e=2).unsqueeze(1)
+                .to_broadcast([P, 8, 24, 2]), op=ALU.mult)
             eng = nc.vector if add_on_v else nc.gpsimd
-            rot = ot[:, :, i, 0:48].rearrange("p h (j e) -> p h j e", e=2)
-            eng.tensor_tensor(out=rot, in0=rot, in1=tb[:, :, :, ::-1], op=ALU.add)
+            rot = ot[:, :, i, 0:48]
+            eng.tensor_tensor(out=rot, in0=rot, in1=tb[:], op=ALU.add)
             store(job)
 
         passed = set()

@@ -36,7 +36,7 @@ V0_STEP = 1
 EARLY_ANGLES = 5
 V1_SKIP = 4
 V1_STEP = 1
-S_RATE = 2.4
+S_RATE = 2.8
 VM_AT = {V0: 4, V1: 16}
 VM_LAST = 21
 V_ADDS = ()

from contextlib import ExitStack
import math

import concourse.mybir as mybir
from concourse.masks import make_identity

FLOPS = 2 * 1024 * 1024 * 3072

F32 = mybir.dt.float32
BF16 = mybir.dt.bfloat16
U32 = mybir.dt.uint32
U8 = mybir.dt.uint8
I32 = mybir.dt.int32
FP8 = mybir.dt.float8_e4m3fn
FP8X4 = mybir.dt.float8_e4m3fn_x4
ALU = mybir.AluOpType
ACT = mybir.ActivationFunctionType

P = 128
NCH = 6
CW = 512
Q0, Q1, K0, K1, V0, V1 = range(NCH)
V_STEPS = {V0: (1, 3, 4), Q1: (4, 5, 6), K0: (8, 10, 12), V1: (15,), K1: (21, 22)}
X_STEPS = (0, 2, 3, 4, 5)
S_BANKS = 4
MM_AHEAD = 3
X_AHEAD = 3
S_FIRST = 8
PASS_FROM = 25
PASS_TO = 32
PASS_LEAD = 1
V1_EARLY = 4
IL_ON_S = ((V1, 0), (V1, 1), (K1, 0))
V0_EARLY = 0
V0_STEP = 1
EARLY_ANGLES = 5
V1_SKIP = 4
V1_STEP = 1
S_RATE = 2.8
VM_AT = {V0: 4, V1: 16}
VM_LAST = 21
V_ADDS = ()
LAST_ADDS = 1
LAST_SPLIT = ((K1, 1),)


def tile_attention_pa_kernel(tc, x, Wqkv_bytes, Wqkv_scale, out_0, out_1, out_2):
    nc = tc.nc
    outs = (out_0, out_1, out_2)
    with ExitStack() as ctx:
        const = ctx.enter_context(tc.tile_pool(name="const", bufs=1))
        xgp = ctx.enter_context(tc.tile_pool(name="xgp", bufs=8))
        wplp = ctx.enter_context(tc.tile_pool(name="wplp", bufs=6))
        wgp = ctx.enter_context(tc.tile_pool(name="wgp", bufs=3))
        otp = ctx.enter_context(tc.tile_pool(name="otp", bufs=6))
        tbp = ctx.enter_context(tc.tile_pool(name="tbp", bufs=6))
        pss = ctx.enter_context(tc.psum_pool(name="pss", bufs=S_BANKS))
        psv = ctx.enter_context(tc.psum_pool(name="psv", bufs=8 - S_BANKS))
        ctx.enter_context(tc.manual_schedule())

        ws = const.tile([P, 2, 4], F32, name="ws")
        nc.scalar.dma_start(out=ws[:], in_=Wqkv_scale.rearrange("(g p t) o -> p g (t o)", p=P, t=4))
        wview = Wqkv_bytes.rearrange("(g p t) n -> g p t n", p=P, t=4)
        wb = []
        for c in range(NCH):
            wb.append(const.tile([P, 2, 4, CW], U8, name="wb%d" % c))
        xsb = []
        for b in range(2):
            xsb.append(const.tile([P, 4, 1024], BF16, name="xsb%d" % b))

        def load_w(c):
            for g in range(2):
                nc.sync.dma_start(out=wb[c][:, g], in_=wview[g][:, :, c * CW:(c + 1) * CW])

        def load_x(b):
            xv = x[b].rearrange("(p i) k -> p i k", i=4)
            for h in range(2):
                nc.sync.dma_start(out=xsb[b][:, 2 * h:2 * h + 2, :], in_=xv[:, 2 * h:2 * h + 2, :])

        load_w(Q0)
        load_x(0)
        load_w(V0)
        load_x(1)
        load_w(Q1)
        for c in (K0, V1, K1):
            load_w(c)

        zero = const.tile([P, 8], F32, name="zero")
        nc.vector.memset(zero[:], 0.0)
        warm = const.tile([P, 8], F32, name="warm")
        nc.scalar.activation(out=warm[:], in_=zero[:], func=ACT.Sin)

        pi = const.tile([P, 1], I32, name="pi")
        nc.gpsimd.iota(pi[:], pattern=[[0, 1]], base=0, channel_multiplier=1)
        fq = const.tile([P, 2, 16], F32, name="fq")
        nc.gpsimd.iota(fq[:, 0, :], pattern=[[127, 8], [0, 2]], base=7, channel_multiplier=0,
                       allow_small_or_imprecise_dtypes=True)
        sg = const.tile([P, 16], F32, name="sg")
        nc.gpsimd.iota(sg[:], pattern=[[0, 8], [2, 2]], base=-1, channel_multiplier=0,
                       allow_small_or_imprecise_dtypes=True)
        i28 = const.tile([P, 4], F32, name="i28")
        nc.gpsimd.iota(i28[:], pattern=[[28, 4]], base=-210, channel_multiplier=0,
                       allow_small_or_imprecise_dtypes=True)
        ident = const.tile([P, P], F32, name="ident")
        make_identity(nc, ident[:])

        idx = const.tile([P, 3], I32, name="idx")
        idf = const.tile([P, 3], F32, name="idf")
        mm = const.tile([P, 6], F32, name="mm")
        nn = const.tile([P, 2, 6, 16], F32, name="nn")
        nflat = nn[:].rearrange("p a s d -> p (a s d)")
        qi = const.tile([P, 192], I32, name="qi")
        rr = const.tile([P, 192], F32, name="rr")
        t1 = const.tile([P, 192], F32, name="t1")
        t2 = const.tile([P, 2, 6, 16], F32, name="t2")
        tabs = []
        for a in range(2):
            tab = const.tile([P, 4, 64], F32, name="tab%d" % a)
            nc.vector.memset(tab[:, :, 48:64], 1.0)
            tabs.append(tab)
        ctab, stab = tabs

        nc.vector.tensor_scalar(out=idx[:, 0:1], in0=pi[:], scalar1=5, scalar2=None,
                                op0=ALU.logical_shift_right)
        nc.vector.tensor_scalar(out=idx[:, 1:2], in0=pi[:], scalar1=2, scalar2=7,
                                op0=ALU.logical_shift_right, op1=ALU.bitwise_and)
        nc.vector.tensor_scalar(out=idx[:, 2:3], in0=pi[:], scalar1=3, scalar2=None,
                                op0=ALU.bitwise_and)
        nc.vector.scalar_tensor_tensor(out=fq[:, 1, :], in0=fq[:, 0, :], scalar=1.0, in1=sg[:],
                                       op0=ALU.mult, op1=ALU.mult)
        nc.vector.tensor_copy(out=idf[:], in_=idx[:])
        nc.vector.tensor_scalar(out=mm[:, 0:1], in0=idf[:, 0:1], scalar1=140.0, scalar2=-210.0,
                                op0=ALU.mult, op1=ALU.add)
        nc.vector.tensor_scalar(out=mm[:, 1:2], in0=idf[:, 1:2], scalar1=60.0, scalar2=-210.0,
                                op0=ALU.mult, op1=ALU.add)
        nc.vector.scalar_tensor_tensor(out=mm[:, 2:6], in0=idf[:, 2:3].to_broadcast([P, 4]),
                                       scalar=112.0, in1=i28[:], op0=ALU.mult, op1=ALU.add)


        angle_steps = [
            lambda: nc.vector.tensor_tensor(
                out=nn[:], in0=mm[:].unsqueeze(1).unsqueeze(3).to_broadcast([P, 2, 6, 16]),
                in1=fq[:].unsqueeze(2).to_broadcast([P, 2, 6, 16]), op=ALU.mult),
            lambda: nc.vector.tensor_scalar(out=nn[:, 0], in0=nn[:, 0], scalar1=191835.0,
                                            scalar2=None, op0=ALU.add),
            lambda: nc.vector.tensor_scalar(out=nn[:, 1], in0=nn[:, 1], scalar1=191100.0,
                                            scalar2=None, op0=ALU.add),
            lambda: nc.vector.tensor_scalar(out=qi[:], in0=nflat, scalar1=1.0 / 2940.0, scalar2=None,
                                            op0=ALU.mult),
            lambda: nc.vector.scalar_tensor_tensor(out=rr[:], in0=qi[:], scalar=-2940.0, in1=nflat,
                                                   op0=ALU.mult, op1=ALU.add),
        ]

        def sines():
            nc.scalar.activation(out=t1[:], in_=rr[:], func=ACT.Abs, bias=-735.0)
            nc.scalar.activation(out=t2[:].rearrange("p a s d -> p (a s d)"), in_=t1[:], func=ACT.Abs,
                                 scale=-1.0, bias=1470.0)
            for a in range(2):
                nc.scalar.activation(out=tabs[a][:, :, 0:32],
                                     in_=t2[:, a, 0:2, :].rearrange("p s d -> p (s d)").unsqueeze(1)
                                     .to_broadcast([P, 4, 32]),
                                     func=ACT.Sin, scale=math.pi / 1470.0, bias=-math.pi / 2)
                nc.scalar.activation(out=tabs[a][:, :, 32:48], in_=t2[:, a, 2:6, :],
                                     func=ACT.Sin, scale=math.pi / 1470.0, bias=-math.pi / 2)

        xc = const.tile([P, 8, 256], U32, name="xc", align_bytes=64)
        xs = const.tile([P, 8, 256], U8, name="xs", align_bytes=64)
        xt = {}
        xg = {}
        quanted = set()

        def x_turn(m):
            words = xsb[m // 4][:, m % 4, :].bitcast(F32)
            bank = pss.tile([P, 4, P], F32, name="sbank")
            for g in range(2):
                for u in range(2):
                    nc.tensor.transpose(bank[:, 2 * g + u, :],
                                        words[:, 256 * g + u:256 * (g + 1):2], ident[:])
            xt[m] = bank

        def x_copy(m):
            xg[m] = xgp.tile([P, 1024], BF16, name="xg", align_bytes=64)
            nc.scalar.copy(out=xg[m][:].bitcast(F32).rearrange("p (g r u) -> p g r u", g=2, u=2),
                           in_=xt[m][:].rearrange("p (g u) r -> p g r u", u=2))

        def x_quant(m):
            nc.vector.quantize_mx(out=xc[:, m, :].bitcast(FP8X4), scales=xs[:, m, :], in_=xg[m][:])
            quanted.add(("x", m))

        wc = []
        wsc = []
        for c in range(NCH):
            wc.append(const.tile([P, 2 * CW], U32, name="wc%d" % c, align_bytes=64))
            wsc.append(const.tile([P, 2 * CW], U8, name="wsc%d" % c, align_bytes=64))
        wpl = {}
        wg = {}
        done = set()
        widened = set()

        def widen(c, g, t, on_v=False):
            if (c, g) not in wpl:
                wpl[(c, g)] = wplp.tile([P, 4, CW], BF16, name="wpl")
            src = wb[c][:, g, t, :].bitcast(FP8)
            col = ws[:, g, t:t + 1]
            if on_v:
                nc.vector.tensor_scalar(out=wpl[(c, g)][:, t, :], in0=src, scalar1=col, scalar2=None,
                                        op0=ALU.mult)
            else:
                nc.scalar.activation(out=wpl[(c, g)][:, t, :], in_=src, func=ACT.Copy, scale=col)
            widened.add((c, g, t))

        def interleave(c, g, on_v):
            if g == 0:
                wg[c] = wgp.tile([P, 2, CW, 4], BF16, name="wg", align_bytes=64)
            copy = nc.vector.tensor_copy if on_v else nc.scalar.copy
            copy(out=wg[c][:, g].rearrange("p (a i) t -> p a t i", i=4),
                 in_=wpl[(c, g)][:].rearrange("p t (a i) -> p a t i", i=4))
            done.add((c, g))

        def w_quant(c):
            nc.vector.quantize_mx(out=wc[c][:].bitcast(FP8X4), scales=wsc[c][:],
                                  in_=wg[c][:].rearrange("p g n t -> p (g n t)"))
            quanted.add(c)

        accs = {}
        ots = {}

        def product(job):
            c, b, i = job
            m = 4 * b + i
            assert {("x", m), c} <= quanted
            if c < V0:
                acc = psv.tile([P, 8, 64], F32, name="acc")
            else:
                acc = pss.tile([P, 8, 64], F32, name="sbank")
            accs[job] = acc
            for g in range(2):
                nc.tensor.matmul_mx(out=acc[:].rearrange("p h d -> p (h d)"),
                                    lhsT=xc[:, m, P * g:P * (g + 1)].bitcast(FP8X4),
                                    lhsT_scale=xs[:, m, P * g:P * (g + 1)],
                                    rhs=wc[c][:, CW * g:CW * (g + 1)].bitcast(FP8X4),
                                    rhs_scale=wsc[c][:, CW * g:CW * (g + 1)],
                                    start=(g == 0), stop=(g == 1))

        def store(job):
            c, b, i = job
            which, half = c // 2, c % 2
            dst = outs[which][b, 8 * half:8 * half + 8].rearrange("h (p i) d -> p h (i d)", i=4)
            src = ots[(c, b)][:].rearrange("p h i d -> p h (i d)")
            if (c, b) in LAST_SPLIT:
                if i % 2 == 1:
                    nc.sync.dma_start(out=dst[:, :, 64 * (i - 1):64 * (i + 1)],
                                      in_=src[:, :, 64 * (i - 1):64 * (i + 1)])
            elif i == 3:
                nc.sync.dma_start(out=dst, in_=src)

        def out_tile(job):
            c, b, i = job
            if (c, b) not in ots:
                ots[(c, b)] = otp.tile([P, 8, 4, 64], F32, name="ot")
            return ots[(c, b)]

        def rotate(job, add_on_v):
            c, b, i = job
            acc = accs[job]
            ot = out_tile(job)
            nd = 48 if job in passed else 64
            nc.vector.tensor_tensor(out=ot[:, :, i, 0:nd], in0=acc[:, :, 0:nd],
                                    in1=ctab[:, i, 0:nd].unsqueeze(1).to_broadcast([P, 8, nd]),
                                    op=ALU.mult)
            tb = tbp.tile([P, 8, 48], F32, name="tb")
            nc.vector.tensor_tensor(
                out=tb[:].rearrange("p h (j e) -> p h j e", e=2),
                in0=acc[:, :, 0:48].rearrange("p h (j e) -> p h j e", e=2)[:, :, :, ::-1],
                in1=stab[:, i, 0:48].rearrange("p (j e) -> p j e", e=2).unsqueeze(1)
                .to_broadcast([P, 8, 24, 2]), op=ALU.mult)
            eng = nc.vector if add_on_v else nc.gpsimd
            rot = ot[:, :, i, 0:48]
            eng.tensor_tensor(out=rot, in0=rot, in1=tb[:], op=ALU.add)
            store(job)

        passed = set()

        def pass_copy(job):
            c, b, i = job
            nc.scalar.copy(out=out_tile(job)[:, :, i, 48:64], in_=accs[job][:, :, 48:64])
            passed.add(job)

        def v_copy(job):
            c, b, i = job
            ot = out_tile(job)
            nc.scalar.copy(out=ot[:, :, i, :], in_=accs[job][:])
            store(job)

        rots = [(c, b, i) for c in (Q0, Q1, K0, K1) for b in range(2) for i in range(4)]

        def widens(c):
            return [(widen, (c, g, t)) for g in range(2) for t in range(4)]

        def v_jobs(c):
            return [(c, b, i) for b in range(2) for i in range(4)]

        def woven(a, b, step):
            out = []
            b = list(b)
            for k in range(len(a)):
                out.append(a[k])
                if k % step == step - 1 and b:
                    out.append(b.pop(0))
            return out + b

        units = woven(widens(V0)[4:] + widens(Q1), [(x_copy, (m,)) for m in range(4, 8)], 2)
        units += [(interleave, (V0, g, False)) for g in range(2) if (V0, g) in IL_ON_S]
        units += woven(widens(K0), [(v_copy, (j,)) for j in v_jobs(V0)[:V0_EARLY]], V0_STEP)
        units += [(interleave, (K0, g, False)) for g in range(2) if (K0, g) in IL_ON_S]
        units += woven(widens(V1), [(v_copy, (j,)) for j in v_jobs(V0)[V0_EARLY:]], V0_STEP)
        units += [(interleave, (V1, g, False)) for g in range(2) if (V1, g) in IL_ON_S]
        units += widens(K1)[:V1_SKIP]
        units += woven(widens(K1)[V1_SKIP:], [(v_copy, (j,)) for j in v_jobs(V1)[:V1_EARLY]], V1_STEP)
        units += [(interleave, (K1, g, False)) for g in range(2) if (K1, g) in IL_ON_S]
        units += [(v_copy, (j,)) for j in v_jobs(V1)[V1_EARLY:]]
        s_at = [0]
        spent = [0.0]

        def ready(fn, args):
            if fn == v_copy:
                return args[0] in accs
            return True

        def s_step():
            fn, args = units[s_at[0]]
            if fn == v_copy and args[0] not in accs:
                product(args[0])
            s_at[0] += 1
            fn(*args)
            spent[0] += 4.5 if fn == interleave else 1.0
            if fn == x_copy and args[0] + X_AHEAD < 8:
                x_turn(args[0] + X_AHEAD)

        def s_until(target):
            while target not in done:
                assert target in IL_ON_S
                s_step()

        def angle():
            if angle_steps:
                angle_steps.pop(0)()

        for n in range(EARLY_ANGLES):
            angle()
        for g in range(2):
            for t in range(2):
                widen(Q0, g, t)
                widen(Q0, g, 2 + t, on_v=True)
                angle()
        for m in range(X_AHEAD):
            x_turn(m)
        interleave(Q0, 0, True)
        angle()
        interleave(Q0, 1, True)
        while angle_steps:
            angle()
        for m in range(4):
            x_copy(m)
            if m + X_AHEAD < 4:
                x_turn(m + X_AHEAD)
        sines()
        for t in range(4):
            widen(V0, 0, t)
        x_quant(0)
        w_quant(Q0)
        for m in range(1, 3):
            x_quant(m)
        issued = [0]

        def issue(upto):
            while issued[0] < min(upto, len(rots)):
                c, b, i = rots[issued[0]]
                if not {("x", 4 * b + i), c} <= quanted:
                    return
                product(rots[issued[0]])
                issued[0] += 1

        issue(2)
        for m in range(4, 4 + X_AHEAD):
            x_turn(m)
        v_products = {}
        for c in (V0, V1):
            for n in range(8):
                v_products.setdefault(min(VM_AT[c] + n, VM_LAST), []).append(v_jobs(c)[n])
        for k in range(len(rots)):
            while s_at[0] < len(units) and spent[0] < S_FIRST + S_RATE * k and ready(*units[s_at[0]]):
                s_step()
            p = k + PASS_LEAD
            if PASS_FROM <= p < min(PASS_TO, issued[0]):
                pass_copy(rots[p])
            rotate(rots[k], k >= len(rots) - LAST_ADDS or k in V_ADDS)
            for m in range(3, 8):
                if X_STEPS[m - 3] == k:
                    while m not in xg:
                        s_step()
                    x_quant(m)
            for c in (V0, Q1, K0, V1, K1):
                steps = V_STEPS[c]
                for n in range(len(steps)):
                    if steps[n] == k:
                        mine = [g for g in range(2) if (c, g) not in IL_ON_S]
                        if n < len(mine):
                            g = mine[n]
                            while (c, g, 3) not in widened:
                                s_step()
                            if g == 1 and (c, 0) in IL_ON_S:
                                s_until((c, 0))
                            interleave(c, g, True)
                        else:
                            for g in range(2):
                                s_until((c, g))
                            w_quant(c)
            for j in v_products.get(k, []):
                if j not in accs:
                    product(j)
            issue(k + 1 + MM_AHEAD)
        while s_at[0] < len(units):
            s_step()
